import numpy as np
import ml_dtypes


def mxq(x, axis, fmt="e4m3"):
    dtype, down = {"e4m3": (ml_dtypes.float8_e4m3fn, 7), "e5m2": (ml_dtypes.float8_e5m2, 14)}[fmt]
    v = np.moveaxis(np.asarray(x, np.float32).astype(ml_dtypes.bfloat16).astype(np.float64), axis, -1)
    blocks = v.reshape(v.shape[:-1] + (-1, 32))
    amax = np.abs(blocks).max(-1, keepdims=True)
    byte = np.maximum(np.where(amax > 0, np.frexp(amax)[1] - 1 + 127, 0) - down, 1)
    scale = np.exp2(byte - 127.0)
    codes = (blocks / scale).astype(np.float32).astype(dtype).astype(np.float64)
    return np.moveaxis((codes * scale).reshape(v.shape), -1, axis)


WIDE = False


def mx_kscale(k):
    if not WIDE:
        return np.ones(k)
    levels = np.array([10, -10, 5, -5, 0])
    a = np.random.permutation(np.resize(levels, k // 512 * 4)).reshape(k // 512, 4)
    idx = np.arange(k)
    return np.exp2(a[idx // 512, idx % 128 // 32])


BF16 = ml_dtypes.bfloat16


def bf(x):
    return np.asarray(x, np.float32).astype(BF16)


def f64(x):
    return np.asarray(x).astype(np.float64)


B, IH, IW, H1, H2, C = 4096, 16, 32, 512, 1024, 10
D = IH * IW
EPS = 1e-5


def batchnorm(v, gamma, beta):
    mu = v.mean(axis=0)
    var = ((v - mu) ** 2).mean(axis=0)
    return gamma * (v - mu) * (1.0 / np.sqrt(var + EPS)) + beta


def setup_inputs():
    s = mx_kscale(D)
    s = s / s.min()
    t = mx_kscale(H1)
    t = t / t.min()
    m1 = (np.resize(s, H1)[:, None] == s[None, :]).astype(np.float64)
    m2 = (np.resize(t, H2)[:, None] == t[None, :]).astype(np.float64)
    return {
        "x": bf(np.random.standard_normal((B, D)) * 8.0 / np.sqrt(D) * s[None, :]),
        "W1": bf(np.random.standard_normal((H1, D)) * 0.05 * m1),
        "g1": bf((1.0 + 0.1 * np.random.standard_normal(H1)) * 8.0 / np.sqrt(H1) * t),
        "b1": bf(np.random.standard_normal(H1) * 2.0 / np.sqrt(H1) * t),
        "W2": bf(np.random.standard_normal((H2, H1)) * 0.05 * m2),
        "g2": bf((1.0 + 0.1 * np.random.standard_normal(H2)) * 8.0 / np.sqrt(H2)),
        "b2": bf(np.random.standard_normal(H2) * 0.1),
    }


def reference(x, W1, g1, b1, W2, g2, b2):
    y1 = mxq(f64(x), 1, "e4m3") @ mxq(np.sign(f64(W1)), 1, "e4m3").T
    h1 = np.maximum(batchnorm(y1, f64(g1), f64(b1)), 0.0)
    y2 = mxq(h1, 1, "e4m3") @ mxq(np.sign(f64(W2)), 1, "e4m3").T
    return batchnorm(np.maximum(y2, 0.0), f64(g2), f64(b2))

@@ -1,0 +1,463 @@
+from contextlib import ExitStack
+
+import concourse.mybir as mybir
+from concourse.masks import make_identity
+
+F32 = mybir.dt.float32
+BF16 = mybir.dt.bfloat16
+U32 = mybir.dt.uint32
+U8 = mybir.dt.uint8
+FP8X4 = mybir.dt.float8_e4m3fn_x4
+ACT = mybir.ActivationFunctionType
+ALU = mybir.AluOpType
+
+P = 128
+PACK = 4
+BATCH, D_IN, H1, H2 = 4096, 512, 512, 1024
+EPS = 1e-5
+CHUNK = 512
+N_CHUNKS = BATCH // CHUNK
+SUB = CHUNK // P
+T1 = H1 // P
+T2 = H2 // P
+PAIR = 2
+N_GROUPS = T2 // PAIR
+N_STEPS = N_GROUPS * N_CHUNKS
+WORDS = D_IN // 2
+STATS = 6
+
+AT_STATS1 = 4
+AT_APPLY1 = AT_STATS1 + N_CHUNKS + 4
+AT_REGROUP = AT_APPLY1 + (T1 - 1) * N_CHUNKS + 1
+AT_RELU2 = AT_REGROUP + 3
+AT_STATS2 = AT_RELU2 + 1
+AT_NORM2 = AT_STATS2 + N_CHUNKS + 1
+AT_STORE = AT_NORM2 + 2
+AT_W1_FIRST = -1
+AT_W1_SECOND = N_CHUNKS + 1
+AT_W2_FIRST = AT_W1_SECOND + 1
+AT_W2_SECOND = AT_REGROUP
+AT_SPLIT = AT_APPLY1
+VECTOR_SHARE = 8
+SCALAR_REGROUP_COLS = 128
+
+
+FLOPS = 2 * BATCH * D_IN * H1 + 2 * BATCH * H1 * H2
+
+
+def tile_binarylinear_pa_t_kernel(tc, x, W1, g1, b1, W2, g2, b2, out):
+    nc = tc.nc
+    with ExitStack() as ctx:
+        ctx.enter_context(tc.manual_schedule())
+        keep = ctx.enter_context(tc.tile_pool(name="keep", bufs=1))
+        psum = ctx.enter_context(tc.psum_pool(name="psum", bufs=8))
+
+        def new_bank(dtype):
+            return psum.tile([P, CHUNK], dtype, name="bank", tag="bank")
+
+        def chunk_cols(c):
+            return slice(c * CHUNK, (c + 1) * CHUNK)
+
+        def tile_cols(t):
+            return slice(t * P, (t + 1) * P)
+
+        vec_rows = keep.tile([P, P], BF16, name="vec_rows")
+        nc.vector.memset(vec_rows[:], 0.0)
+        first_row = {}
+        row = 0
+        for key, vec in (("g1", g1), ("b1", b1), ("g2", g2), ("b2", b2)):
+            n_rows = vec.shape[0] // P
+            nc.scalar.dma_start(
+                out=vec_rows[row : row + n_rows, :], in_=vec.rearrange("(r c) -> r c", c=P)
+            )
+            first_row[key] = row
+            row += n_rows
+        n_vec_rows = row
+        vecs = keep.tile([P, n_vec_rows], F32, name="vecs")
+        neg_vecs = keep.tile([P, n_vec_rows], F32, name="neg_vecs")
+
+        eps = keep.tile([P, 1], F32, name="eps")
+        nc.vector.memset(eps[:], EPS)
+        warm = keep.tile([P, 1], F32, name="warm")
+        nc.scalar.activation(out=warm[:], in_=eps[:], func=ACT.Sqrt)
+
+        ident_f = keep.tile([P, P], F32, name="ident_f")
+        make_identity(nc, ident_f[:])
+        ident_b = keep.tile([P, P], BF16, name="ident_b")
+        make_identity(nc, ident_b[:])
+
+        w1_sb = keep.tile([P, T1 * D_IN], BF16, name="w1_sb")
+        w2_sb = keep.tile([P, T2 * H1], BF16, name="w2_sb")
+        w2_grouped = keep.tile([P, PACK * H2], BF16, name="w2_grouped", align_bytes=64)
+        w1_codes = keep.tile([P, H1], U32, name="w1_codes", align_bytes=64)
+        w1_scales = keep.tile([P, H1], U8, name="w1_scales", align_bytes=64)
+        w2_codes = keep.tile([P, H2], U32, name="w2_codes", align_bytes=64)
+        w2_scales = keep.tile([P, H2], U8, name="w2_scales", align_bytes=64)
+        x_codes = keep.tile([P, BATCH], U32, name="x_codes", align_bytes=64)
+        x_scales = keep.tile([P, BATCH], U8, name="x_scales", align_bytes=64)
+        h_codes = keep.tile([P, BATCH], U32, name="h_codes", align_bytes=64)
+        h_scales = keep.tile([P, BATCH], U8, name="h_scales", align_bytes=64)
+        stats1 = keep.tile([P, T1, N_CHUNKS, STATS], F32, name="stats1")
+        stats2 = keep.tile([P, T2, N_CHUNKS, STATS], F32, name="stats2")
+        h_planes = keep.tile([P, T1, BATCH], BF16, name="h_planes")
+
+        pools = {}
+        banks = {}
+        norms = {}
+
+        def transpose_words(words, half):
+            bank = new_bank(F32)
+            for tt in range(2):
+                for u in range(2):
+                    src = (2 * half + tt) * WORDS + u * P
+                    dst = u * 2 * P + tt * P
+                    nc.tensor.transpose(
+                        out=bank[:, dst : dst + P],
+                        in_=words[:, src : src + P],
+                        identity=ident_f[:],
+                    )
+            return bank
+
+        def norm_vectors(layer, first, n):
+            g_col = first_row["g%d" % layer] + first
+            b_col = first_row["b%d" % layer] + first
+            return vecs[:, g_col : g_col + n], neg_vecs[:, g_col : g_col + n], vecs[:, b_col : b_col + n]
+
+        def norm_moments(layer, stats, first, n):
+            label = "%d_%d" % (layer, first)
+            neg_gamma = norm_vectors(layer, first, n)[1]
+            mean_var = keep.tile([P, n, 2], F32, name="mean_var_" + label)
+            for i in range(n):
+                nc.vector.bn_aggr(
+                    out=mean_var[:, i, :],
+                    in_=stats[:, first + i, :, :].rearrange("p c s -> p (c s)"),
+                )
+            neg_gamma_mean = keep.tile([P, n], F32, name="neg_gamma_mean_" + label)
+            nc.vector.tensor_mul(out=neg_gamma_mean[:], in0=neg_gamma, in1=mean_var[:, :, 0])
+            norms[(layer, first)] = (mean_var, neg_gamma_mean)
+
+        def norm_std(layer, first, n):
+            mean_var, neg_gamma_mean = norms[(layer, first)]
+            std = keep.tile([P, n], F32, name="std_%d_%d" % (layer, first))
+            nc.scalar.activation(out=std[:], in_=mean_var[:, :, 1], func=ACT.Sqrt, bias=eps[:])
+            norms[(layer, first)] = (std, neg_gamma_mean)
+
+        def norm_rstd(layer, first, n):
+            std, neg_gamma_mean = norms[(layer, first)]
+            rstd = keep.tile([P, n], F32, name="rstd_%d_%d" % (layer, first))
+            nc.vector.reciprocal(out=rstd[:], in_=std[:])
+            norms[(layer, first)] = (rstd, neg_gamma_mean)
+
+        def norm_gain_shift(layer, first, n):
+            label = "%d_%d" % (layer, first)
+            gamma, neg_gamma, beta = norm_vectors(layer, first, n)
+            rstd, neg_gamma_mean = norms[(layer, first)]
+            gain = keep.tile([P, n], F32, name="gain_" + label)
+            nc.vector.tensor_mul(out=gain[:], in0=gamma, in1=rstd[:])
+            shift = keep.tile([P, n], F32, name="shift_" + label)
+            for i in range(n):
+                nc.vector.tensor_scalar(
+                    out=shift[:, i : i + 1],
+                    in0=rstd[:, i : i + 1],
+                    scalar1=neg_gamma_mean[:, i : i + 1],
+                    scalar2=beta[:, i : i + 1],
+                    op0=ALU.mult,
+                    op1=ALU.add,
+                )
+            norms[(layer, first)] = (gain, shift)
+
+        def layer1_norm(stage, item):
+            if 0 <= item < T1 * N_CHUNKS and item % N_CHUNKS == N_CHUNKS - 1:
+                stage(1, item // N_CHUNKS, 1)
+
+        def layer2_norm_chain(stage, item):
+            if 0 <= item < N_STEPS and item % N_CHUNKS == N_CHUNKS - 1:
+                stage(2, (item // N_CHUNKS) * PAIR, PAIR)
+
+        x_sb = {}
+        x_grouped = {}
+
+        def w1_prepare(now, half):
+            if now != 0:
+                return
+            cols = slice(half * 2 * P, (half + 1) * 2 * P)
+            bank = transpose_words(w1_sb[:].bitcast(F32), half)
+            grouped = pools["x"].tile(
+                [P, PACK * 2 * P], BF16, name="w1_grouped%d" % half, align_bytes=64
+            )
+            nc.scalar.activation(
+                out=grouped[:].rearrange("p (w u e) -> p w u e", u=2, e=2),
+                in_=bank[:].bitcast(BF16).rearrange("p (u w e) -> p w u e", u=2, e=2),
+                func=ACT.Sign,
+            )
+            nc.vector.quantize_mx(
+                out=w1_codes[:, cols].bitcast(FP8X4), scales=w1_scales[:, cols], in_=grouped[:]
+            )
+
+        def x_transpose(c):
+            if not 0 <= c < N_CHUNKS:
+                return
+            words = x_sb[c][:].bitcast(F32)
+            banks[("x", c)] = [transpose_words(words, half) for half in range(2)]
+
+        def x_copy(c):
+            if not 0 <= c < N_CHUNKS:
+                return
+            grouped = pools["xg"].tile(
+                [P, PACK * CHUNK], BF16, name="x_grouped", tag="x_grouped", align_bytes=64
+            )
+            for half in range(2):
+                dst = (
+                    grouped[:]
+                    .bitcast(F32)[:, half * CHUNK : (half + 1) * CHUNK]
+                    .rearrange("p (w u) -> p w u", u=2)
+                )
+                src = banks[("x", c)][half][:].rearrange("p (u w) -> p w u", u=2)
+                nc.scalar.copy(out=dst, in_=src)
+            x_grouped[c] = grouped
+
+        def x_quantise(c):
+            if not 0 <= c < N_CHUNKS:
+                return
+            nc.vector.quantize_mx(
+                out=x_codes[:, chunk_cols(c)].bitcast(FP8X4),
+                scales=x_scales[:, chunk_cols(c)],
+                in_=x_grouped[c][:],
+            )
+
+        def w2_sign(m, first, last):
+            if not first <= m < last:
+                return
+            bank = new_bank(BF16)
+            for t in range(PACK):
+                nc.tensor.transpose(
+                    out=bank[:, tile_cols(t)],
+                    in_=w2_sb[:, m * H1 + t * P : m * H1 + (t + 1) * P],
+                    identity=ident_b[:],
+                )
+            nc.scalar.activation(
+                out=w2_grouped[:, m * PACK * P : (m + 1) * PACK * P],
+                in_=bank[:].rearrange("p (t f) -> p f t", t=PACK),
+                func=ACT.Sign,
+            )
+            if m == last - 1:
+                nc.vector.quantize_mx(
+                    out=w2_codes[:, first * P : last * P].bitcast(FP8X4),
+                    scales=w2_scales[:, first * P : last * P],
+                    in_=w2_grouped[:, first * PACK * P : last * PACK * P],
+                )
+
+        def layer1_matmul(stage, item):
+            if not 0 <= item < T1 * N_CHUNKS:
+                return
+            t, c = divmod(item, N_CHUNKS)
+            bank = new_bank(F32)
+            nc.tensor.matmul_mx(
+                out=bank[:],
+                lhsT=w1_codes[:, tile_cols(t)].bitcast(FP8X4),
+                lhsT_scale=w1_scales[:, tile_cols(t)],
+                rhs=x_codes[:, chunk_cols(c)].bitcast(FP8X4),
+                rhs_scale=x_scales[:, chunk_cols(c)],
+                start=True,
+                stop=True,
+            )
+            banks[(stage, item)] = bank
+
+        def layer1_stats(item):
+            if not 0 <= item < T1 * N_CHUNKS:
+                return
+            t, c = divmod(item, N_CHUNKS)
+            nc.vector.bn_stats(out=stats1[:, t, c, :], in_=banks[("stats1", item)][:])
+            if c == N_CHUNKS - 1:
+                norm_moments(1, stats1, t, 1)
+
+        def layer1_apply(item):
+            if not 0 <= item < T1 * N_CHUNKS:
+                return
+            t, c = divmod(item, N_CHUNKS)
+            gain, shift = norms[(1, t)]
+            nc.scalar.activation(
+                out=h_planes[:, t, chunk_cols(c)],
+                in_=banks[("apply1", item)][:],
+                func=ACT.Relu,
+                scale=gain[:],
+                bias=shift[:],
+            )
+
+        h_grouped = {}
+
+        def h_regroup(c):
+            if not 0 <= c < N_CHUNKS:
+                return
+            grouped = pools["hg"].tile(
+                [P, PACK * CHUNK], BF16, name="h_grouped", tag="h_grouped", align_bytes=64
+            )
+            dst = grouped[:].rearrange("p (c i t) -> p c t i", i=4, t=PACK)
+            src = h_planes[:, :, chunk_cols(c)].rearrange("p t (c i) -> p c t i", i=4)
+            cut = (CHUNK - SCALAR_REGROUP_COLS) // 4
+            nc.vector.tensor_copy(out=dst[:, :cut], in_=src[:, :cut])
+            nc.scalar.copy(out=dst[:, cut:], in_=src[:, cut:])
+            h_grouped[c] = grouped
+
+        def h_quantise(c):
+            if not 0 <= c < N_CHUNKS:
+                return
+            nc.vector.quantize_mx(
+                out=h_codes[:, chunk_cols(c)].bitcast(FP8X4),
+                scales=h_scales[:, chunk_cols(c)],
+                in_=h_grouped[c][:],
+            )
+
+        relu_y2 = {}
+
+        def layer2_matmul(item):
+            if not 0 <= item < N_STEPS:
+                return
+            group, c = divmod(item, N_CHUNKS)
+            banks[("y2", item)] = []
+            for m in range(group * PAIR, (group + 1) * PAIR):
+                bank = new_bank(F32)
+                nc.tensor.matmul_mx(
+                    out=bank[:],
+                    lhsT=w2_codes[:, tile_cols(m)].bitcast(FP8X4),
+                    lhsT_scale=w2_scales[:, tile_cols(m)],
+                    rhs=h_codes[:, chunk_cols(c)].bitcast(FP8X4),
+                    rhs_scale=h_scales[:, chunk_cols(c)],
+                    start=True,
+                    stop=True,
+                )
+                banks[("y2", item)].append(bank)
+
+        def layer2_relu(item):
+            if not 0 <= item < N_STEPS:
+                return
+            group, c = divmod(item, N_CHUNKS)
+            for i in range(PAIR):
+                m = group * PAIR + i
+                if c == 0:
+                    relu_y2[m] = pools["r"].tile([P, BATCH], F32, name="relu_y2", tag="relu_y2")
+                nc.scalar.activation(
+                    out=relu_y2[m][:, chunk_cols(c)], in_=banks[("y2", item)][i][:], func=ACT.Relu
+                )
+
+        def layer2_stats(item):
+            if not 0 <= item < N_STEPS:
+                return
+            group, c = divmod(item, N_CHUNKS)
+            for m in range(group * PAIR, (group + 1) * PAIR):
+                nc.vector.bn_stats(out=stats2[:, m, c, :], in_=relu_y2[m][:, chunk_cols(c)])
+            if c == N_CHUNKS - 1:
+                norm_moments(2, stats2, group * PAIR, PAIR)
+
+        def layer2_norm(item):
+            if not 0 <= item < N_STEPS:
+                return
+            group, c = divmod(item, N_CHUNKS)
+            gain, shift = norms[(2, group * PAIR)]
+            for i in range(PAIR):
+                piece = relu_y2[group * PAIR + i][:, chunk_cols(c)]
+                nc.vector.tensor_scalar(
+                    out=piece,
+                    in0=piece,
+                    scalar1=gain[:, i : i + 1],
+                    scalar2=shift[:, i : i + 1],
+                    op0=ALU.mult,
+                    op1=ALU.add,
+                )
+
+        def layer2_transpose(item):
+            if not 0 <= item < N_STEPS:
+                return
+            group, c = divmod(item, N_CHUNKS)
+            banks[("out", item)] = []
+            for half in range(2):
+                bank = new_bank(F32)
+                for jj in range(2):
+                    col = c * CHUNK + (2 * half + jj) * P
+                    for i in range(PAIR):
+                        dst = (jj * PAIR + i) * P
+                        nc.tensor.transpose(
+                            out=bank[:, dst : dst + P],
+                            in_=relu_y2[group * PAIR + i][:, col : col + P],
+                            identity=ident_f[:],
+                        )
+                banks[("out", item)].append(bank)
+
+        def layer2_store(item):
+            if not 0 <= item < N_STEPS:
+                return
+            group, c = divmod(item, N_CHUNKS)
+            staged = pools["o"].tile([P, SUB * PAIR * P], F32, name="staged", tag="staged")
+            for half in range(2):
+                dst = staged[:, half * CHUNK : (half + 1) * CHUNK]
+                if (2 * item + half) % VECTOR_SHARE == VECTOR_SHARE - 1:
+                    nc.vector.tensor_copy(out=dst, in_=banks[("out", item)][half][:])
+                else:
+                    nc.scalar.copy(out=dst, in_=banks[("out", item)][half][:])
+            f0 = group * PAIR * P
+            nc.sync.dma_start(
+                out=out[chunk_cols(c), f0 : f0 + PAIR * P].rearrange("(p j) f -> p j f", j=SUB),
+                in_=staged[:].rearrange("p (j f) -> p j f", j=SUB),
+            )
+
+        def step(n):
+            layer2_norm_chain(norm_std, n - AT_STATS2 - 1)
+            layer2_relu(n - AT_RELU2)
+            layer2_store(n - AT_STORE)
+            layer1_norm(norm_std, n - AT_STATS1 - 1)
+            layer1_apply(n - AT_APPLY1)
+            x_copy(n - 1)
+            layer2_norm_chain(norm_gain_shift, n - AT_STATS2 - 2)
+            layer2_norm(n - AT_NORM2)
+            layer1_norm(norm_gain_shift, n - AT_STATS1 - 3)
+            h_regroup(n - AT_REGROUP)
+            layer1_stats(n - AT_STATS1)
+            layer2_stats(n - AT_STATS2)
+            layer1_norm(norm_rstd, n - AT_STATS1 - 2)
+            layer2_norm_chain(norm_rstd, n - AT_STATS2 - 1)
+            x_quantise(n - 2)
+            h_quantise(n - AT_REGROUP - 1)
+            w1_prepare(n - AT_W1_FIRST, 0)
+            w1_prepare(n - AT_W1_SECOND, 1)
+            x_transpose(n)
+            layer1_matmul("stats1", n - AT_STATS1 + 1)
+            layer1_matmul("apply1", n - AT_APPLY1 + 1)
+            w2_sign(n - AT_W2_FIRST, 0, T2 // 2)
+            w2_sign(n - AT_W2_SECOND + T2 // 2, T2 // 2, T2)
+            layer2_matmul(n - AT_RELU2 + 1)
+            layer2_transpose(n - AT_STORE + 1)
+
+        with ExitStack() as first_part:
+            pools["x"] = first_part.enter_context(tc.tile_pool(name="x_pool", bufs=1))
+            pools["xg"] = first_part.enter_context(tc.tile_pool(name="xg_pool", bufs=3))
+            nc.sync.dma_start(
+                out=w1_sb[:].rearrange("p (t k) -> p t k", t=T1),
+                in_=W1.rearrange("(t p) k -> p t k", p=P),
+            )
+            for c in range(N_CHUNKS):
+                x_sb[c] = pools["x"].tile([P, SUB * D_IN], BF16, name="x_sb%d" % c)
+                nc.sync.dma_start(
+                    out=x_sb[c][:],
+                    in_=x[chunk_cols(c), :].rearrange("(p j) k -> p (j k)", j=SUB),
+                )
+            for half in range(2):
+                rows = slice(half * H2 // 2, (half + 1) * H2 // 2)
+                nc.sync.dma_start(
+                    out=w2_sb[:, half * T2 // 2 * H1 : (half + 1) * T2 // 2 * H1].rearrange(
+                        "p (m k) -> p m k", k=H1
+                    ),
+                    in_=W2[rows, :].rearrange("(m p) k -> p m k", p=P),
+                )
+            for n in range(-1, AT_SPLIT):
+                step(n)
+                if n == 0:
+                    vec_bank = new_bank(BF16)
+                    nc.tensor.transpose(out=vec_bank[:, 0:P], in_=vec_rows[:], identity=ident_b[:])
+                    nc.vector.tensor_copy(out=vecs[:], in_=vec_bank[:, 0:n_vec_rows])
+                    nc.vector.tensor_scalar_mul(out=neg_vecs[:], in0=vec_bank[:, 0:n_vec_rows], scalar1=-1.0)
+
+        pools["hg"] = ctx.enter_context(tc.tile_pool(name="hg_pool", bufs=2))
+        pools["r"] = ctx.enter_context(tc.tile_pool(name="r_pool", bufs=3 * PAIR))
+        pools["o"] = ctx.enter_context(tc.tile_pool(name="o_pool", bufs=4))
+        for n in range(AT_SPLIT, AT_STORE + N_STEPS):
+            step(n)

@@ -38,7 +38,7 @@ AT_W1_SECOND = N_CHUNKS + 1
 AT_W2_FIRST = AT_W1_SECOND + 1
 AT_W2_SECOND = AT_REGROUP
 AT_SPLIT = AT_APPLY1
-VECTOR_SHARE = 8
+VECTOR_SHARE = 2
 SCALAR_REGROUP_COLS = 128
 
 
@@ -356,7 +356,8 @@ def tile_binarylinear_pa_t_kernel(tc, x, W1, g1, b1, W2, g2, b2, out):
             gain, shift = norms[(2, group * PAIR)]
             for i in range(PAIR):
                 piece = relu_y2[group * PAIR + i][:, chunk_cols(c)]
-                nc.vector.tensor_scalar(
+                engine = nc.vector if group == N_GROUPS - 1 else nc.gpsimd
+                engine.tensor_scalar(
                     out=piece,
                     in0=piece,
                     scalar1=gain[:, i : i + 1],

@@ -48,7 +48,6 @@ FLOPS = 2 * BATCH * D_IN * H1 + 2 * BATCH * H1 * H2
 def tile_binarylinear_pa_t_kernel(tc, x, W1, g1, b1, W2, g2, b2, out):
     nc = tc.nc
     with ExitStack() as ctx:
-        ctx.enter_context(tc.manual_schedule())
         keep = ctx.enter_context(tc.tile_pool(name="keep", bufs=1))
         psum = ctx.enter_context(tc.psum_pool(name="psum", bufs=8))
 

@@ -38,7 +38,7 @@ AT_W1_SECOND = N_CHUNKS + 1
 AT_W2_FIRST = AT_W1_SECOND + 1
 AT_W2_SECOND = AT_REGROUP
 AT_SPLIT = AT_APPLY1
-VECTOR_SHARE = 2
+VECTOR_SHARE = 3
 SCALAR_REGROUP_COLS = 128
 
 

@@ -20,27 +20,24 @@ N_CHUNKS = BATCH // CHUNK
 SUB = CHUNK // P
 T1 = H1 // P
 T2 = H2 // P
-PAIR = 2
-N_GROUPS = T2 // PAIR
-N_STEPS = N_GROUPS * N_CHUNKS
 WORDS = D_IN // 2
 STATS = 6
 
-AT_STATS1 = 4
-AT_APPLY1 = AT_STATS1 + N_CHUNKS + 4
-AT_REGROUP = AT_APPLY1 + (T1 - 1) * N_CHUNKS + 1
-AT_RELU2 = AT_REGROUP + 3
-AT_STATS2 = AT_RELU2 + 1
-AT_NORM2 = AT_STATS2 + N_CHUNKS + 1
-AT_STORE = AT_NORM2 + 2
-AT_W1_FIRST = -1
-AT_W1_SECOND = N_CHUNKS + 1
-AT_W2_FIRST = AT_W1_SECOND + 1
-AT_W2_SECOND = AT_REGROUP
-AT_SPLIT = AT_APPLY1
-VECTOR_SHARE = 3
-SCALAR_REGROUP_COLS = 128
 
+QUARTERS = N_CHUNKS // 2
+
+AT_STATS1 = 2
+AT_STATS1_LATE = AT_STATS1 + N_CHUNKS
+AT_W1_SECOND = N_CHUNKS
+AT_W2_SIGN = N_CHUNKS
+AT_APPLY1 = AT_STATS1_LATE + 3
+VECTOR_APPLIES = 4
+AT_APPLY1_LATE = AT_APPLY1 + 3 * N_CHUNKS - VECTOR_APPLIES
+AT_REGROUP = AT_APPLY1_LATE + 1
+AT_LAYER2 = AT_REGROUP + 3
+NO_RELU = T2 * QUARTERS - 11
+NO_STATS = T2 * QUARTERS - 7
+SCALAR_REGROUP_COLS = 128
 
 FLOPS = 2 * BATCH * D_IN * H1 + 2 * BATCH * H1 * H2
 
@@ -48,6 +45,7 @@ FLOPS = 2 * BATCH * D_IN * H1 + 2 * BATCH * H1 * H2
 def tile_binarylinear_pa_t_kernel(tc, x, W1, g1, b1, W2, g2, b2, out):
     nc = tc.nc
     with ExitStack() as ctx:
+        ctx.enter_context(tc.manual_schedule())
         keep = ctx.enter_context(tc.tile_pool(name="keep", bufs=1))
         psum = ctx.enter_context(tc.psum_pool(name="psum", bufs=8))
 
@@ -74,19 +72,38 @@ def tile_binarylinear_pa_t_kernel(tc, x, W1, g1, b1, W2, g2, b2, out):
         n_vec_rows = row
         vecs = keep.tile([P, n_vec_rows], F32, name="vecs")
         neg_vecs = keep.tile([P, n_vec_rows], F32, name="neg_vecs")
-
-        eps = keep.tile([P, 1], F32, name="eps")
-        nc.vector.memset(eps[:], EPS)
+        minus_half = keep.tile([P, 1], F32, name="minus_half")
+        nc.vector.memset(minus_half[:], -0.5)
         warm = keep.tile([P, 1], F32, name="warm")
-        nc.scalar.activation(out=warm[:], in_=eps[:], func=ACT.Sqrt)
+        nc.scalar.activation(out=warm[:], in_=minus_half[:], func=ACT.Sign)
 
         ident_f = keep.tile([P, P], F32, name="ident_f")
         make_identity(nc, ident_f[:])
         ident_b = keep.tile([P, P], BF16, name="ident_b")
         make_identity(nc, ident_b[:])
 
-        w1_sb = keep.tile([P, T1 * D_IN], BF16, name="w1_sb")
-        w2_sb = keep.tile([P, T2 * H1], BF16, name="w2_sb")
+        big = ctx.enter_context(tc.tile_pool(name="big", bufs=6))
+        grouped_pool = ctx.enter_context(tc.tile_pool(name="grouped", bufs=4))
+        staged_pool = ctx.enter_context(tc.tile_pool(name="staged", bufs=4))
+
+        def new_grouped():
+            return grouped_pool.tile(
+                [P, PACK * CHUNK], BF16, name="grouped", tag="grouped", align_bytes=64
+            )
+
+        weights = big.tile([P, (T1 + T2) * D_IN], BF16, name="weights", tag="big")
+        w1_sb = weights[:, 0 : T1 * D_IN]
+        w2_sb = weights[:, T1 * D_IN : (T1 + T2) * D_IN]
+        x_tiles = []
+        for half in range(2):
+            x_half = big.tile([P, N_CHUNKS // 2 * SUB * D_IN], BF16, name="x_half", tag="big")
+            x_tiles.append(x_half)
+
+        def x_rows(c):
+            i = c % (N_CHUNKS // 2)
+            return x_tiles[c // (N_CHUNKS // 2)][:, i * SUB * D_IN : (i + 1) * SUB * D_IN]
+
+        w1_grouped = keep.tile([P, PACK * H1], BF16, name="w1_grouped", align_bytes=64)
         w2_grouped = keep.tile([P, PACK * H2], BF16, name="w2_grouped", align_bytes=64)
         w1_codes = keep.tile([P, H1], U32, name="w1_codes", align_bytes=64)
         w1_scales = keep.tile([P, H1], U8, name="w1_scales", align_bytes=64)
@@ -100,9 +117,11 @@ def tile_binarylinear_pa_t_kernel(tc, x, W1, g1, b1, W2, g2, b2, out):
         stats2 = keep.tile([P, T2, N_CHUNKS, STATS], F32, name="stats2")
         h_planes = keep.tile([P, T1, BATCH], BF16, name="h_planes")
 
-        pools = {}
         banks = {}
         norms = {}
+        x_grouped = {}
+        h_grouped = {}
+        relu_y2 = {}
 
         def transpose_words(words, half):
             bank = new_bank(F32)
@@ -117,94 +136,68 @@ def tile_binarylinear_pa_t_kernel(tc, x, W1, g1, b1, W2, g2, b2, out):
                     )
             return bank
 
-        def norm_vectors(layer, first, n):
-            g_col = first_row["g%d" % layer] + first
-            b_col = first_row["b%d" % layer] + first
-            return vecs[:, g_col : g_col + n], neg_vecs[:, g_col : g_col + n], vecs[:, b_col : b_col + n]
-
-        def norm_moments(layer, stats, first, n):
-            label = "%d_%d" % (layer, first)
-            neg_gamma = norm_vectors(layer, first, n)[1]
-            mean_var = keep.tile([P, n, 2], F32, name="mean_var_" + label)
-            for i in range(n):
-                nc.vector.bn_aggr(
-                    out=mean_var[:, i, :],
-                    in_=stats[:, first + i, :, :].rearrange("p c s -> p (c s)"),
-                )
-            neg_gamma_mean = keep.tile([P, n], F32, name="neg_gamma_mean_" + label)
-            nc.vector.tensor_mul(out=neg_gamma_mean[:], in0=neg_gamma, in1=mean_var[:, :, 0])
-            norms[(layer, first)] = (mean_var, neg_gamma_mean)
-
-        def norm_std(layer, first, n):
-            mean_var, neg_gamma_mean = norms[(layer, first)]
-            std = keep.tile([P, n], F32, name="std_%d_%d" % (layer, first))
-            nc.scalar.activation(out=std[:], in_=mean_var[:, :, 1], func=ACT.Sqrt, bias=eps[:])
-            norms[(layer, first)] = (std, neg_gamma_mean)
-
-        def norm_rstd(layer, first, n):
-            std, neg_gamma_mean = norms[(layer, first)]
-            rstd = keep.tile([P, n], F32, name="rstd_%d_%d" % (layer, first))
-            nc.vector.reciprocal(out=rstd[:], in_=std[:])
-            norms[(layer, first)] = (rstd, neg_gamma_mean)
-
-        def norm_gain_shift(layer, first, n):
-            label = "%d_%d" % (layer, first)
-            gamma, neg_gamma, beta = norm_vectors(layer, first, n)
-            rstd, neg_gamma_mean = norms[(layer, first)]
-            gain = keep.tile([P, n], F32, name="gain_" + label)
-            nc.vector.tensor_mul(out=gain[:], in0=gamma, in1=rstd[:])
-            shift = keep.tile([P, n], F32, name="shift_" + label)
-            for i in range(n):
-                nc.vector.tensor_scalar(
-                    out=shift[:, i : i + 1],
-                    in0=rstd[:, i : i + 1],
-                    scalar1=neg_gamma_mean[:, i : i + 1],
-                    scalar2=beta[:, i : i + 1],
-                    op0=ALU.mult,
-                    op1=ALU.add,
-                )
-            norms[(layer, first)] = (gain, shift)
-
-        def layer1_norm(stage, item):
-            if 0 <= item < T1 * N_CHUNKS and item % N_CHUNKS == N_CHUNKS - 1:
-                stage(1, item // N_CHUNKS, 1)
-
-        def layer2_norm_chain(stage, item):
-            if 0 <= item < N_STEPS and item % N_CHUNKS == N_CHUNKS - 1:
-                stage(2, (item // N_CHUNKS) * PAIR, PAIR)
-
-        x_sb = {}
-        x_grouped = {}
-
-        def w1_prepare(now, half):
-            if now != 0:
-                return
-            cols = slice(half * 2 * P, (half + 1) * 2 * P)
-            bank = transpose_words(w1_sb[:].bitcast(F32), half)
-            grouped = pools["x"].tile(
-                [P, PACK * 2 * P], BF16, name="w1_grouped%d" % half, align_bytes=64
+        def norm_moments(layer, stats, tile):
+            mean_var = keep.tile([P, 2], F32, name="mean_var_%d_%d" % (layer, tile))
+            nc.vector.bn_aggr(
+                out=mean_var[:], in_=stats[:, tile, :, :].rearrange("p c s -> p (c s)")
             )
+            norms[(layer, tile)] = mean_var
+
+        def norm_gain_shift(layer, tile):
+            label = "%d_%d" % (layer, tile)
+            g_col = first_row["g%d" % layer] + tile
+            b_col = first_row["b%d" % layer] + tile
+            gamma, neg_gamma = vecs[:, g_col : g_col + 1], neg_vecs[:, g_col : g_col + 1]
+            mean_var = norms[(layer, tile)]
+            var_eps = keep.tile([P, 1], F32, name="var_eps_" + label)
+            nc.gpsimd.tensor_scalar(
+                out=var_eps[:], in0=mean_var[:, 1:2], scalar1=EPS, scalar2=0.0, op0=ALU.add, op1=ALU.add
+            )
+            gamma_mean = keep.tile([P, 1], F32, name="gamma_mean_" + label)
+            nc.gpsimd.tensor_tensor(out=gamma_mean[:], in0=mean_var[:, 0:1], in1=neg_gamma, op=ALU.mult)
+            rstd = keep.tile([P, 1], F32, name="rstd_" + label)
+            nc.gpsimd.tensor_tensor(out=rstd[:], in0=var_eps[:], in1=minus_half[:], op=ALU.pow)
+            gain = keep.tile([P, 1], F32, name="gain_" + label)
+            nc.gpsimd.tensor_tensor(out=gain[:], in0=rstd[:], in1=gamma, op=ALU.mult)
+            shift = keep.tile([P, 1], F32, name="shift_" + label)
+            nc.gpsimd.tensor_scalar(
+                out=shift[:],
+                in0=rstd[:],
+                scalar1=gamma_mean[:],
+                scalar2=vecs[:, b_col : b_col + 1],
+                op0=ALU.mult,
+                op1=ALU.add,
+            )
+            norms[(layer, tile)] = (gain, shift)
+
+        def w1_transpose(half):
+            banks[("w1", half)] = transpose_words(w1_sb.bitcast(F32), half)
+
+        def w1_sign(half):
+            width = 2 * P
             nc.scalar.activation(
-                out=grouped[:].rearrange("p (w u e) -> p w u e", u=2, e=2),
-                in_=bank[:].bitcast(BF16).rearrange("p (u w e) -> p w u e", u=2, e=2),
+                out=w1_grouped[:, half * PACK * width : (half + 1) * PACK * width].rearrange(
+                    "p (w u e) -> p w u e", u=2, e=2
+                ),
+                in_=banks[("w1", half)][:].bitcast(BF16).rearrange("p (u w e) -> p w u e", u=2, e=2),
                 func=ACT.Sign,
             )
+
+        def w1_quantise(half):
+            width = 2 * P
+            cols = slice(half * width, (half + 1) * width)
             nc.vector.quantize_mx(
-                out=w1_codes[:, cols].bitcast(FP8X4), scales=w1_scales[:, cols], in_=grouped[:]
+                out=w1_codes[:, cols].bitcast(FP8X4),
+                scales=w1_scales[:, cols],
+                in_=w1_grouped[:, half * PACK * width : (half + 1) * PACK * width],
             )
 
         def x_transpose(c):
-            if not 0 <= c < N_CHUNKS:
-                return
-            words = x_sb[c][:].bitcast(F32)
+            words = x_rows(c).bitcast(F32)
             banks[("x", c)] = [transpose_words(words, half) for half in range(2)]
 
         def x_copy(c):
-            if not 0 <= c < N_CHUNKS:
-                return
-            grouped = pools["xg"].tile(
-                [P, PACK * CHUNK], BF16, name="x_grouped", tag="x_grouped", align_bytes=64
-            )
+            grouped = new_grouped()
             for half in range(2):
                 dst = (
                     grouped[:]
@@ -216,17 +209,13 @@ def tile_binarylinear_pa_t_kernel(tc, x, W1, g1, b1, W2, g2, b2, out):
             x_grouped[c] = grouped
 
         def x_quantise(c):
-            if not 0 <= c < N_CHUNKS:
-                return
             nc.vector.quantize_mx(
                 out=x_codes[:, chunk_cols(c)].bitcast(FP8X4),
                 scales=x_scales[:, chunk_cols(c)],
                 in_=x_grouped[c][:],
             )
 
-        def w2_sign(m, first, last):
-            if not first <= m < last:
-                return
+        def w2_transpose(m):
             bank = new_bank(BF16)
             for t in range(PACK):
                 nc.tensor.transpose(
@@ -234,22 +223,24 @@ def tile_binarylinear_pa_t_kernel(tc, x, W1, g1, b1, W2, g2, b2, out):
                     in_=w2_sb[:, m * H1 + t * P : m * H1 + (t + 1) * P],
                     identity=ident_b[:],
                 )
+            banks[("w2", m)] = bank
+
+        def w2_sign(m):
             nc.scalar.activation(
                 out=w2_grouped[:, m * PACK * P : (m + 1) * PACK * P],
-                in_=bank[:].rearrange("p (t f) -> p f t", t=PACK),
+                in_=banks[("w2", m)][:].rearrange("p (t f) -> p f t", t=PACK),
                 func=ACT.Sign,
             )
-            if m == last - 1:
-                nc.vector.quantize_mx(
-                    out=w2_codes[:, first * P : last * P].bitcast(FP8X4),
-                    scales=w2_scales[:, first * P : last * P],
-                    in_=w2_grouped[:, first * PACK * P : last * PACK * P],
-                )
 
-        def layer1_matmul(stage, item):
-            if not 0 <= item < T1 * N_CHUNKS:
-                return
-            t, c = divmod(item, N_CHUNKS)
+        def w2_quantise(half):
+            first, last = half * T2 // 2, (half + 1) * T2 // 2
+            nc.vector.quantize_mx(
+                out=w2_codes[:, first * P : last * P].bitcast(FP8X4),
+                scales=w2_scales[:, first * P : last * P],
+                in_=w2_grouped[:, first * PACK * P : last * PACK * P],
+            )
+
+        def layer1_matmul(use, t, c):
             bank = new_bank(F32)
             nc.tensor.matmul_mx(
                 out=bank[:],
@@ -260,61 +251,45 @@ def tile_binarylinear_pa_t_kernel(tc, x, W1, g1, b1, W2, g2, b2, out):
                 start=True,
                 stop=True,
             )
-            banks[(stage, item)] = bank
+            banks[(use, t, c)] = bank
 
-        def layer1_stats(item):
-            if not 0 <= item < T1 * N_CHUNKS:
-                return
-            t, c = divmod(item, N_CHUNKS)
-            nc.vector.bn_stats(out=stats1[:, t, c, :], in_=banks[("stats1", item)][:])
+        def layer1_stats(t, c):
+            nc.vector.bn_stats(out=stats1[:, t, c, :], in_=banks[("stats1", t, c)][:])
             if c == N_CHUNKS - 1:
-                norm_moments(1, stats1, t, 1)
+                norm_moments(1, stats1, t)
 
-        def layer1_apply(item):
-            if not 0 <= item < T1 * N_CHUNKS:
-                return
-            t, c = divmod(item, N_CHUNKS)
+        def layer1_apply(t, c, on_vector):
             gain, shift = norms[(1, t)]
-            nc.scalar.activation(
-                out=h_planes[:, t, chunk_cols(c)],
-                in_=banks[("apply1", item)][:],
-                func=ACT.Relu,
-                scale=gain[:],
-                bias=shift[:],
-            )
-
-        h_grouped = {}
+            dst = h_planes[:, t, chunk_cols(c)]
+            src = banks[("apply1", t, c)][:]
+            if on_vector:
+                nc.vector.tensor_scalar(
+                    out=dst, in0=src, scalar1=gain[:], scalar2=shift[:], op0=ALU.mult, op1=ALU.add
+                )
+            else:
+                nc.scalar.activation(out=dst, in_=src, func=ACT.Relu, scale=gain[:], bias=shift[:])
 
         def h_regroup(c):
-            if not 0 <= c < N_CHUNKS:
-                return
-            grouped = pools["hg"].tile(
-                [P, PACK * CHUNK], BF16, name="h_grouped", tag="h_grouped", align_bytes=64
-            )
+            grouped = new_grouped()
             dst = grouped[:].rearrange("p (c i t) -> p c t i", i=4, t=PACK)
             src = h_planes[:, :, chunk_cols(c)].rearrange("p t (c i) -> p c t i", i=4)
             cut = (CHUNK - SCALAR_REGROUP_COLS) // 4
-            nc.vector.tensor_copy(out=dst[:, :cut], in_=src[:, :cut])
-            nc.scalar.copy(out=dst[:, cut:], in_=src[:, cut:])
+            nc.vector.tensor_scalar_max(out=dst[:, :cut], in0=src[:, :cut], scalar1=0.0)
+            nc.scalar.activation(out=dst[:, cut:], in_=src[:, cut:], func=ACT.Relu)
             h_grouped[c] = grouped
 
         def h_quantise(c):
-            if not 0 <= c < N_CHUNKS:
-                return
             nc.vector.quantize_mx(
                 out=h_codes[:, chunk_cols(c)].bitcast(FP8X4),
                 scales=h_scales[:, chunk_cols(c)],
                 in_=h_grouped[c][:],
             )
 
-        relu_y2 = {}
+        def quarter_chunks(q):
+            return (2 * q, 2 * q + 1)
 
-        def layer2_matmul(item):
-            if not 0 <= item < N_STEPS:
-                return
-            group, c = divmod(item, N_CHUNKS)
-            banks[("y2", item)] = []
-            for m in range(group * PAIR, (group + 1) * PAIR):
+        def layer2_matmul(m, q):
+            for c in quarter_chunks(q):
                 bank = new_bank(F32)
                 nc.tensor.matmul_mx(
                     out=bank[:],
@@ -325,139 +300,147 @@ def tile_binarylinear_pa_t_kernel(tc, x, W1, g1, b1, W2, g2, b2, out):
                     start=True,
                     stop=True,
                 )
-                banks[("y2", item)].append(bank)
+                banks[("y2", m, c)] = bank
 
-        def layer2_relu(item):
-            if not 0 <= item < N_STEPS:
-                return
-            group, c = divmod(item, N_CHUNKS)
-            for i in range(PAIR):
-                m = group * PAIR + i
-                if c == 0:
-                    relu_y2[m] = pools["r"].tile([P, BATCH], F32, name="relu_y2", tag="relu_y2")
+        def layer2_relu(m, q):
+            if q == 0:
+                relu_tile = big.tile([P, BATCH], F32, name="relu_tile", tag="big")
+                relu_y2[m] = relu_tile
+            for c in quarter_chunks(q):
                 nc.scalar.activation(
-                    out=relu_y2[m][:, chunk_cols(c)], in_=banks[("y2", item)][i][:], func=ACT.Relu
+                    out=relu_y2[m][:, chunk_cols(c)], in_=banks[("y2", m, c)][:], func=ACT.Relu
                 )
 
-        def layer2_stats(item):
-            if not 0 <= item < N_STEPS:
-                return
-            group, c = divmod(item, N_CHUNKS)
-            for m in range(group * PAIR, (group + 1) * PAIR):
+        def layer2_stats(m, q):
+            for c in quarter_chunks(q):
                 nc.vector.bn_stats(out=stats2[:, m, c, :], in_=relu_y2[m][:, chunk_cols(c)])
-            if c == N_CHUNKS - 1:
-                norm_moments(2, stats2, group * PAIR, PAIR)
+            if q == QUARTERS - 1:
+                norm_moments(2, stats2, m)
 
-        def layer2_norm(item):
-            if not 0 <= item < N_STEPS:
-                return
-            group, c = divmod(item, N_CHUNKS)
-            gain, shift = norms[(2, group * PAIR)]
-            for i in range(PAIR):
-                piece = relu_y2[group * PAIR + i][:, chunk_cols(c)]
-                engine = nc.vector if group == N_GROUPS - 1 else nc.gpsimd
-                engine.tensor_scalar(
-                    out=piece,
-                    in0=piece,
-                    scalar1=gain[:, i : i + 1],
-                    scalar2=shift[:, i : i + 1],
-                    op0=ALU.mult,
-                    op1=ALU.add,
-                )
+        def layer2_norm(m, q):
+            gain, shift = norms[(2, m)]
+            piece = relu_y2[m][:, 2 * q * CHUNK : 2 * (q + 1) * CHUNK]
+            engine = nc.vector if m == T2 - 1 else nc.gpsimd
+            engine.tensor_scalar(
+                out=piece, in0=piece, scalar1=gain[:], scalar2=shift[:], op0=ALU.mult, op1=ALU.add
+            )
 
-        def layer2_transpose(item):
-            if not 0 <= item < N_STEPS:
-                return
-            group, c = divmod(item, N_CHUNKS)
-            banks[("out", item)] = []
-            for half in range(2):
+        def layer2_transpose(m, q):
+            for c in quarter_chunks(q):
                 bank = new_bank(F32)
-                for jj in range(2):
-                    col = c * CHUNK + (2 * half + jj) * P
-                    for i in range(PAIR):
-                        dst = (jj * PAIR + i) * P
-                        nc.tensor.transpose(
-                            out=bank[:, dst : dst + P],
-                            in_=relu_y2[group * PAIR + i][:, col : col + P],
-                            identity=ident_f[:],
-                        )
-                banks[("out", item)].append(bank)
+                for j in range(SUB):
+                    col = c * CHUNK + j * P
+                    nc.tensor.transpose(
+                        out=bank[:, tile_cols(j)],
+                        in_=relu_y2[m][:, col : col + P],
+                        identity=ident_f[:],
+                    )
+                banks[("out", m, c)] = bank
 
-        def layer2_store(item):
-            if not 0 <= item < N_STEPS:
-                return
-            group, c = divmod(item, N_CHUNKS)
-            staged = pools["o"].tile([P, SUB * PAIR * P], F32, name="staged", tag="staged")
-            for half in range(2):
-                dst = staged[:, half * CHUNK : (half + 1) * CHUNK]
-                if (2 * item + half) % VECTOR_SHARE == VECTOR_SHARE - 1:
-                    nc.vector.tensor_copy(out=dst, in_=banks[("out", item)][half][:])
+        def layer2_store(m, q):
+            staged = staged_pool.tile([P, 2 * CHUNK], F32, name="staged", tag="staged")
+            for i, c in enumerate(quarter_chunks(q)):
+                dst = staged[:, i * CHUNK : (i + 1) * CHUNK]
+                if i == 1 and not NO_RELU <= m * QUARTERS + q < NO_STATS:
+                    nc.vector.tensor_copy(out=dst, in_=banks[("out", m, c)][:])
                 else:
-                    nc.scalar.copy(out=dst, in_=banks[("out", item)][half][:])
-            f0 = group * PAIR * P
+                    nc.scalar.copy(out=dst, in_=banks[("out", m, c)][:])
+                nc.sync.dma_start(
+                    out=out[chunk_cols(c), tile_cols(m)].rearrange("(p j) f -> p j f", j=SUB),
+                    in_=staged[:, i * CHUNK : (i + 1) * CHUNK].rearrange("p (j f) -> p j f", j=SUB),
+                )
+
+        def load_w1(half):
+            rows = slice(half * H1 // 2, (half + 1) * H1 // 2)
+            cols = slice(half * T1 // 2 * D_IN, (half + 1) * T1 // 2 * D_IN)
             nc.sync.dma_start(
-                out=out[chunk_cols(c), f0 : f0 + PAIR * P].rearrange("(p j) f -> p j f", j=SUB),
-                in_=staged[:].rearrange("p (j f) -> p j f", j=SUB),
+                out=w1_sb[:, cols].rearrange("p (t k) -> p t k", k=D_IN),
+                in_=W1[rows, :].rearrange("(t p) k -> p t k", p=P),
             )
 
-        def step(n):
-            layer2_norm_chain(norm_std, n - AT_STATS2 - 1)
-            layer2_relu(n - AT_RELU2)
-            layer2_store(n - AT_STORE)
-            layer1_norm(norm_std, n - AT_STATS1 - 1)
-            layer1_apply(n - AT_APPLY1)
-            x_copy(n - 1)
-            layer2_norm_chain(norm_gain_shift, n - AT_STATS2 - 2)
-            layer2_norm(n - AT_NORM2)
-            layer1_norm(norm_gain_shift, n - AT_STATS1 - 3)
-            h_regroup(n - AT_REGROUP)
-            layer1_stats(n - AT_STATS1)
-            layer2_stats(n - AT_STATS2)
-            layer1_norm(norm_rstd, n - AT_STATS1 - 2)
-            layer2_norm_chain(norm_rstd, n - AT_STATS2 - 1)
-            x_quantise(n - 2)
-            h_quantise(n - AT_REGROUP - 1)
-            w1_prepare(n - AT_W1_FIRST, 0)
-            w1_prepare(n - AT_W1_SECOND, 1)
-            x_transpose(n)
-            layer1_matmul("stats1", n - AT_STATS1 + 1)
-            layer1_matmul("apply1", n - AT_APPLY1 + 1)
-            w2_sign(n - AT_W2_FIRST, 0, T2 // 2)
-            w2_sign(n - AT_W2_SECOND + T2 // 2, T2 // 2, T2)
-            layer2_matmul(n - AT_RELU2 + 1)
-            layer2_transpose(n - AT_STORE + 1)
-
-        with ExitStack() as first_part:
-            pools["x"] = first_part.enter_context(tc.tile_pool(name="x_pool", bufs=1))
-            pools["xg"] = first_part.enter_context(tc.tile_pool(name="xg_pool", bufs=3))
+        def load_x(c):
             nc.sync.dma_start(
-                out=w1_sb[:].rearrange("p (t k) -> p t k", t=T1),
-                in_=W1.rearrange("(t p) k -> p t k", p=P),
+                out=x_rows(c), in_=x[chunk_cols(c), :].rearrange("(p j) k -> p (j k)", j=SUB)
             )
+
+        def load_w2(half):
+            rows = slice(half * H2 // 2, (half + 1) * H2 // 2)
+            cols = slice(half * T2 // 2 * H1, (half + 1) * T2 // 2 * H1)
+            nc.sync.dma_start(
+                out=w2_sb[:, cols].rearrange("p (m k) -> p m k", k=H1),
+                in_=W2[rows, :].rearrange("(m p) k -> p m k", p=P),
+            )
+
+        load_w1(0)
+        for c in range(N_CHUNKS):
+            load_x(c)
+        load_w1(1)
+        load_w2(0)
+        load_w2(1)
+
+        LANES = (
+            "matmul1", "x_transpose", "w_transpose",
+            "store", "relu2", "apply1", "x_copy", "sign", "norm2", "gain_shift", "regroup",
+            "quantise", "stats1", "stats2", "matmul2", "transpose2",
+        )
+        agenda = {}
+
+        def at(slot, lane, call, *args):
+            agenda.setdefault(slot, []).append((LANES.index(lane), call, args))
+
+        def vectors():
+            vec_bank = new_bank(BF16)
+            nc.tensor.transpose(out=vec_bank[:, 0:P], in_=vec_rows[:], identity=ident_b[:])
+            nc.vector.tensor_copy(out=vecs[:], in_=vec_bank[:, 0:n_vec_rows])
+            nc.vector.tensor_scalar_mul(out=neg_vecs[:], in0=vec_bank[:, 0:n_vec_rows], scalar1=-1.0)
+
+        for half, slot in enumerate((-1, AT_W1_SECOND)):
+            at(slot, "w_transpose", w1_transpose, half)
+            at(slot, "sign", w1_sign, half)
+            at(slot + half, "quantise", w1_quantise, half)
+        at(5, "w_transpose", vectors)
+        for c in range(N_CHUNKS):
+            at(c, "x_transpose", x_transpose, c)
+            at(c, "x_copy", x_copy, c)
+            at(c + 1, "quantise", x_quantise, c)
+        for m in range(T2):
+            at(AT_W2_SIGN + m // 2, "w_transpose", w2_transpose, m)
+            at(AT_W2_SIGN + m // 2, "sign", w2_sign, m)
+            if m % (T2 // 2) == T2 // 2 - 1:
+                at(AT_W2_SIGN + m // 2 + 2, "quantise", w2_quantise, m // (T2 // 2))
+        for t in range(T1):
             for c in range(N_CHUNKS):
-                x_sb[c] = pools["x"].tile([P, SUB * D_IN], BF16, name="x_sb%d" % c)
-                nc.sync.dma_start(
-                    out=x_sb[c][:],
-                    in_=x[chunk_cols(c), :].rearrange("(p j) k -> p (j k)", j=SUB),
-                )
-            for half in range(2):
-                rows = slice(half * H2 // 2, (half + 1) * H2 // 2)
-                nc.sync.dma_start(
-                    out=w2_sb[:, half * T2 // 2 * H1 : (half + 1) * T2 // 2 * H1].rearrange(
-                        "p (m k) -> p m k", k=H1
-                    ),
-                    in_=W2[rows, :].rearrange("(m p) k -> p m k", p=P),
-                )
-            for n in range(-1, AT_SPLIT):
-                step(n)
-                if n == 0:
-                    vec_bank = new_bank(BF16)
-                    nc.tensor.transpose(out=vec_bank[:, 0:P], in_=vec_rows[:], identity=ident_b[:])
-                    nc.vector.tensor_copy(out=vecs[:], in_=vec_bank[:, 0:n_vec_rows])
-                    nc.vector.tensor_scalar_mul(out=neg_vecs[:], in0=vec_bank[:, 0:n_vec_rows], scalar1=-1.0)
+                slot = AT_STATS1 + c if t < 2 else AT_STATS1_LATE + (t - 2) * N_CHUNKS + c
+                at(slot, "matmul1", layer1_matmul, "stats1", t, c)
+                at(slot, "stats1", layer1_stats, t, c)
+                if c == N_CHUNKS - 1:
+                    at(slot + 1, "gain_shift", norm_gain_shift, 1, t)
+                on_vector = t == 2 and c < VECTOR_APPLIES
+                if t < 3:
+                    slot = AT_APPLY1 + t * N_CHUNKS + c - (VECTOR_APPLIES if t == 2 else 0)
+                else:
+                    slot = AT_APPLY1_LATE + c
+                if on_vector:
+                    slot = AT_STATS1_LATE + 2 * N_CHUNKS + c // 2
+                at(slot, "matmul1", layer1_matmul, "apply1", t, c)
+                at(slot, "apply1", layer1_apply, t, c, on_vector)
+        for c in range(N_CHUNKS):
+            at(AT_REGROUP + c, "regroup", h_regroup, c)
+            at(AT_REGROUP + c + 1, "quantise", h_quantise, c)
+        for m in range(T2):
+            for q in range(QUARTERS):
+                relu_at = AT_LAYER2 + (2 * q + m if m < 2 else m * QUARTERS + q)
+                stats_at = AT_LAYER2 + (2 * q + 1 if m == 0 else (m + 1) * QUARTERS + q)
+                norm_at = AT_LAYER2 + (m + 2) * QUARTERS + 2 + q
+                at(relu_at - 1, "matmul2", layer2_matmul, m, q)
+                at(relu_at, "relu2", layer2_relu, m, q)
+                at(stats_at, "stats2", layer2_stats, m, q)
+                if q == QUARTERS - 1:
+                    at(stats_at + 1, "gain_shift", norm_gain_shift, 2, m)
+                at(norm_at if m < T2 - 1 else norm_at - q, "norm2", layer2_norm, m, q)
+                at(norm_at + 1, "transpose2", layer2_transpose, m, q)
+                at(norm_at + 2, "store", layer2_store, m, q)
 
-        pools["hg"] = ctx.enter_context(tc.tile_pool(name="hg_pool", bufs=2))
-        pools["r"] = ctx.enter_context(tc.tile_pool(name="r_pool", bufs=3 * PAIR))
-        pools["o"] = ctx.enter_context(tc.tile_pool(name="o_pool", bufs=4))
-        for n in range(AT_SPLIT, AT_STORE + N_STEPS):
-            step(n)
+        for slot in sorted(agenda):
+            for lane, call, args in sorted(agenda[slot], key=lambda entry: entry[0]):
+                call(*args)

@@ -24,7 +24,8 @@ WORDS = D_IN // 2
 STATS = 6
 
 
-QUARTERS = N_CHUNKS // 2
+PAIR = 2
+N_GROUPS = T2 // PAIR
 
 AT_STATS1 = 2
 AT_STATS1_LATE = AT_STATS1 + N_CHUNKS
@@ -34,9 +35,9 @@ AT_APPLY1 = AT_STATS1_LATE + 3
 VECTOR_APPLIES = 4
 AT_APPLY1_LATE = AT_APPLY1 + 3 * N_CHUNKS - VECTOR_APPLIES
 AT_REGROUP = AT_APPLY1_LATE + 1
-AT_LAYER2 = AT_REGROUP + 3
-NO_RELU = T2 * QUARTERS - 11
-NO_STATS = T2 * QUARTERS - 7
+AT_LAYER2 = AT_REGROUP + 2
+LAG_NORM = 3
+LAG_TR = 2
 SCALAR_REGROUP_COLS = 128
 
 FLOPS = 2 * BATCH * D_IN * H1 + 2 * BATCH * H1 * H2
@@ -72,10 +73,10 @@ def tile_binarylinear_pa_t_kernel(tc, x, W1, g1, b1, W2, g2, b2, out):
         n_vec_rows = row
         vecs = keep.tile([P, n_vec_rows], F32, name="vecs")
         neg_vecs = keep.tile([P, n_vec_rows], F32, name="neg_vecs")
-        minus_half = keep.tile([P, 1], F32, name="minus_half")
+        minus_half = keep.tile([P, PAIR], F32, name="minus_half")
         nc.vector.memset(minus_half[:], -0.5)
         warm = keep.tile([P, 1], F32, name="warm")
-        nc.scalar.activation(out=warm[:], in_=minus_half[:], func=ACT.Sign)
+        nc.scalar.activation(out=warm[:], in_=minus_half[:, 0:1], func=ACT.Sign)
 
         ident_f = keep.tile([P, P], F32, name="ident_f")
         make_identity(nc, ident_f[:])
@@ -136,39 +137,42 @@ def tile_binarylinear_pa_t_kernel(tc, x, W1, g1, b1, W2, g2, b2, out):
                     )
             return bank
 
-        def norm_moments(layer, stats, tile):
-            mean_var = keep.tile([P, 2], F32, name="mean_var_%d_%d" % (layer, tile))
-            nc.vector.bn_aggr(
-                out=mean_var[:], in_=stats[:, tile, :, :].rearrange("p c s -> p (c s)")
-            )
-            norms[(layer, tile)] = mean_var
+        def norm_moments(layer, stats, first, n):
+            mean_var = keep.tile([P, n, 2], F32, name="mean_var_%d_%d" % (layer, first))
+            for i in range(n):
+                nc.vector.bn_aggr(
+                    out=mean_var[:, i, :],
+                    in_=stats[:, first + i, :, :].rearrange("p c s -> p (c s)"),
+                )
+            norms[(layer, first)] = mean_var
 
-        def norm_gain_shift(layer, tile):
-            label = "%d_%d" % (layer, tile)
-            g_col = first_row["g%d" % layer] + tile
-            b_col = first_row["b%d" % layer] + tile
-            gamma, neg_gamma = vecs[:, g_col : g_col + 1], neg_vecs[:, g_col : g_col + 1]
-            mean_var = norms[(layer, tile)]
-            var_eps = keep.tile([P, 1], F32, name="var_eps_" + label)
+        def norm_gain_shift(layer, first, n):
+            label = "%d_%d" % (layer, first)
+            g_col = first_row["g%d" % layer] + first
+            b_col = first_row["b%d" % layer] + first
+            gamma, neg_gamma = vecs[:, g_col : g_col + n], neg_vecs[:, g_col : g_col + n]
+            mean_var = norms[(layer, first)]
+            var_eps = keep.tile([P, n], F32, name="var_eps_" + label)
             nc.gpsimd.tensor_scalar(
-                out=var_eps[:], in0=mean_var[:, 1:2], scalar1=EPS, scalar2=0.0, op0=ALU.add, op1=ALU.add
+                out=var_eps[:], in0=mean_var[:, :, 1], scalar1=EPS, scalar2=0.0, op0=ALU.add, op1=ALU.add
             )
-            gamma_mean = keep.tile([P, 1], F32, name="gamma_mean_" + label)
-            nc.gpsimd.tensor_tensor(out=gamma_mean[:], in0=mean_var[:, 0:1], in1=neg_gamma, op=ALU.mult)
-            rstd = keep.tile([P, 1], F32, name="rstd_" + label)
-            nc.gpsimd.tensor_tensor(out=rstd[:], in0=var_eps[:], in1=minus_half[:], op=ALU.pow)
-            gain = keep.tile([P, 1], F32, name="gain_" + label)
+            gamma_mean = keep.tile([P, n], F32, name="gamma_mean_" + label)
+            nc.gpsimd.tensor_tensor(out=gamma_mean[:], in0=mean_var[:, :, 0], in1=neg_gamma, op=ALU.mult)
+            rstd = keep.tile([P, n], F32, name="rstd_" + label)
+            nc.gpsimd.tensor_tensor(out=rstd[:], in0=var_eps[:], in1=minus_half[:, 0:n], op=ALU.pow)
+            gain = keep.tile([P, n], F32, name="gain_" + label)
             nc.gpsimd.tensor_tensor(out=gain[:], in0=rstd[:], in1=gamma, op=ALU.mult)
-            shift = keep.tile([P, 1], F32, name="shift_" + label)
-            nc.gpsimd.tensor_scalar(
-                out=shift[:],
-                in0=rstd[:],
-                scalar1=gamma_mean[:],
-                scalar2=vecs[:, b_col : b_col + 1],
-                op0=ALU.mult,
-                op1=ALU.add,
-            )
-            norms[(layer, tile)] = (gain, shift)
+            shift = keep.tile([P, n], F32, name="shift_" + label)
+            for i in range(n):
+                nc.gpsimd.tensor_scalar(
+                    out=shift[:, i : i + 1],
+                    in0=rstd[:, i : i + 1],
+                    scalar1=gamma_mean[:, i : i + 1],
+                    scalar2=vecs[:, b_col + i : b_col + i + 1],
+                    op0=ALU.mult,
+                    op1=ALU.add,
+                )
+            norms[(layer, first)] = (gain, shift)
 
         def w1_transpose(half):
             banks[("w1", half)] = transpose_words(w1_sb.bitcast(F32), half)
@@ -256,7 +260,7 @@ def tile_binarylinear_pa_t_kernel(tc, x, W1, g1, b1, W2, g2, b2, out):
         def layer1_stats(t, c):
             nc.vector.bn_stats(out=stats1[:, t, c, :], in_=banks[("stats1", t, c)][:])
             if c == N_CHUNKS - 1:
-                norm_moments(1, stats1, t)
+                norm_moments(1, stats1, t, 1)
 
         def layer1_apply(t, c, on_vector):
             gain, shift = norms[(1, t)]
@@ -285,11 +289,11 @@ def tile_binarylinear_pa_t_kernel(tc, x, W1, g1, b1, W2, g2, b2, out):
                 in_=h_grouped[c][:],
             )
 
-        def quarter_chunks(q):
-            return (2 * q, 2 * q + 1)
+        def group_tiles(g):
+            return range(g * PAIR, (g + 1) * PAIR)
 
-        def layer2_matmul(m, q):
-            for c in quarter_chunks(q):
+        def layer2_matmul(g, c):
+            for m in group_tiles(g):
                 bank = new_bank(F32)
                 nc.tensor.matmul_mx(
                     out=bank[:],
@@ -302,53 +306,57 @@ def tile_binarylinear_pa_t_kernel(tc, x, W1, g1, b1, W2, g2, b2, out):
                 )
                 banks[("y2", m, c)] = bank
 
-        def layer2_relu(m, q):
-            if q == 0:
-                relu_tile = big.tile([P, BATCH], F32, name="relu_tile", tag="big")
-                relu_y2[m] = relu_tile
-            for c in quarter_chunks(q):
+        def layer2_relu(g, c):
+            for m in group_tiles(g):
+                if c == 0:
+                    relu_tile = big.tile([P, BATCH], F32, name="relu_tile", tag="big")
+                    relu_y2[m] = relu_tile
                 nc.scalar.activation(
                     out=relu_y2[m][:, chunk_cols(c)], in_=banks[("y2", m, c)][:], func=ACT.Relu
                 )
 
-        def layer2_stats(m, q):
-            for c in quarter_chunks(q):
+        def layer2_stats(g, c):
+            for m in group_tiles(g):
                 nc.vector.bn_stats(out=stats2[:, m, c, :], in_=relu_y2[m][:, chunk_cols(c)])
-            if q == QUARTERS - 1:
-                norm_moments(2, stats2, m)
+            if c == N_CHUNKS - 1:
+                norm_moments(2, stats2, g * PAIR, PAIR)
 
-        def layer2_norm(m, q):
-            gain, shift = norms[(2, m)]
-            piece = relu_y2[m][:, 2 * q * CHUNK : 2 * (q + 1) * CHUNK]
-            engine = nc.vector if m == T2 - 1 else nc.gpsimd
-            engine.tensor_scalar(
-                out=piece, in0=piece, scalar1=gain[:], scalar2=shift[:], op0=ALU.mult, op1=ALU.add
-            )
-
-        def layer2_transpose(m, q):
-            for c in quarter_chunks(q):
-                bank = new_bank(F32)
-                for j in range(SUB):
-                    col = c * CHUNK + j * P
-                    nc.tensor.transpose(
-                        out=bank[:, tile_cols(j)],
-                        in_=relu_y2[m][:, col : col + P],
-                        identity=ident_f[:],
-                    )
-                banks[("out", m, c)] = bank
-
-        def layer2_store(m, q):
-            staged = staged_pool.tile([P, 2 * CHUNK], F32, name="staged", tag="staged")
-            for i, c in enumerate(quarter_chunks(q)):
-                dst = staged[:, i * CHUNK : (i + 1) * CHUNK]
-                if i == 1 and not NO_RELU <= m * QUARTERS + q < NO_STATS:
-                    nc.vector.tensor_copy(out=dst, in_=banks[("out", m, c)][:])
-                else:
-                    nc.scalar.copy(out=dst, in_=banks[("out", m, c)][:])
-                nc.sync.dma_start(
-                    out=out[chunk_cols(c), tile_cols(m)].rearrange("(p j) f -> p j f", j=SUB),
-                    in_=staged[:, i * CHUNK : (i + 1) * CHUNK].rearrange("p (j f) -> p j f", j=SUB),
+        def layer2_norm(g, c):
+            gain, shift = norms[(2, g * PAIR)]
+            for i, m in enumerate(group_tiles(g)):
+                piece = relu_y2[m][:, c * CHUNK : (c + 2) * CHUNK]
+                engine = nc.vector if g == N_GROUPS - 1 else nc.gpsimd
+                engine.tensor_scalar(
+                    out=piece,
+                    in0=piece,
+                    scalar1=gain[:, i : i + 1],
+                    scalar2=shift[:, i : i + 1],
+                    op0=ALU.mult,
+                    op1=ALU.add,
                 )
+
+        def layer2_transpose(g, c):
+            for half in range(2):
+                bank = new_bank(F32)
+                for jj in range(2):
+                    col = c * CHUNK + (2 * half + jj) * P
+                    for i, m in enumerate(group_tiles(g)):
+                        nc.tensor.transpose(
+                            out=bank[:, tile_cols(jj * PAIR + i)],
+                            in_=relu_y2[m][:, col : col + P],
+                            identity=ident_f[:],
+                        )
+                banks[("out", g, c, half)] = bank
+
+        def layer2_store(g, c):
+            staged = staged_pool.tile([P, SUB * PAIR * P], F32, name="staged", tag="staged")
+            nc.scalar.copy(out=staged[:, 0:CHUNK], in_=banks[("out", g, c, 0)][:])
+            nc.vector.tensor_copy(out=staged[:, CHUNK : 2 * CHUNK], in_=banks[("out", g, c, 1)][:])
+            f0 = g * PAIR * P
+            nc.sync.dma_start(
+                out=out[chunk_cols(c), f0 : f0 + PAIR * P].rearrange("(p j) f -> p j f", j=SUB),
+                in_=staged[:].rearrange("p (j f) -> p j f", j=SUB),
+            )
 
         def load_w1(half):
             rows = slice(half * H1 // 2, (half + 1) * H1 // 2)
@@ -414,7 +422,7 @@ def tile_binarylinear_pa_t_kernel(tc, x, W1, g1, b1, W2, g2, b2, out):
                 at(slot, "matmul1", layer1_matmul, "stats1", t, c)
                 at(slot, "stats1", layer1_stats, t, c)
                 if c == N_CHUNKS - 1:
-                    at(slot + 1, "gain_shift", norm_gain_shift, 1, t)
+                    at(slot + 1, "gain_shift", norm_gain_shift, 1, t, 1)
                 on_vector = t == 2 and c < VECTOR_APPLIES
                 if t < 3:
                     slot = AT_APPLY1 + t * N_CHUNKS + c - (VECTOR_APPLIES if t == 2 else 0)
@@ -427,19 +435,19 @@ def tile_binarylinear_pa_t_kernel(tc, x, W1, g1, b1, W2, g2, b2, out):
         for c in range(N_CHUNKS):
             at(AT_REGROUP + c, "regroup", h_regroup, c)
             at(AT_REGROUP + c + 1, "quantise", h_quantise, c)
-        for m in range(T2):
-            for q in range(QUARTERS):
-                relu_at = AT_LAYER2 + (2 * q + m if m < 2 else m * QUARTERS + q)
-                stats_at = AT_LAYER2 + (2 * q + 1 if m == 0 else (m + 1) * QUARTERS + q)
-                norm_at = AT_LAYER2 + (m + 2) * QUARTERS + 2 + q
-                at(relu_at - 1, "matmul2", layer2_matmul, m, q)
-                at(relu_at, "relu2", layer2_relu, m, q)
-                at(stats_at, "stats2", layer2_stats, m, q)
-                if q == QUARTERS - 1:
-                    at(stats_at + 1, "gain_shift", norm_gain_shift, 2, m)
-                at(norm_at if m < T2 - 1 else norm_at - q, "norm2", layer2_norm, m, q)
-                at(norm_at + 1, "transpose2", layer2_transpose, m, q)
-                at(norm_at + 2, "store", layer2_store, m, q)
+        for g in range(N_GROUPS):
+            for c in range(N_CHUNKS):
+                slot = AT_LAYER2 + g * N_CHUNKS + c
+                at(slot - 1, "matmul2", layer2_matmul, g, c)
+                at(slot, "relu2", layer2_relu, g, c)
+                at(slot + 1, "stats2", layer2_stats, g, c)
+                if c == N_CHUNKS - 1:
+                    at(slot + 2, "gain_shift", norm_gain_shift, 2, g * PAIR, PAIR)
+                slot += N_CHUNKS + LAG_NORM
+                if c % 2 == 0:
+                    at(slot, "norm2", layer2_norm, g, c)
+                at(slot + LAG_TR, "transpose2", layer2_transpose, g, c)
+                at(slot + LAG_TR + 1, "store", layer2_store, g, c)
 
         for slot in sorted(agenda):
             for lane, call, args in sorted(agenda[slot], key=lambda entry: entry[0]):

@@ -124,6 +124,16 @@ def tile_binarylinear_pa_t_kernel(tc, x, W1, g1, b1, W2, g2, b2, out):
         h_grouped = {}
         relu_y2 = {}
 
+        zeros = keep.tile([P, CHUNK], BF16, name="zeros")
+        nc.vector.memset(zeros[:], 0.0)
+
+        def keep_warm(n):
+            bank = new_bank(F32)
+            for i in range(n):
+                nc.tensor.matmul(
+                    out=bank[:], lhsT=zeros[:, 0:P], rhs=zeros[:], start=True, stop=True
+                )
+
         def transpose_words(words, half):
             bank = new_bank(F32)
             for tt in range(2):
@@ -387,7 +397,7 @@ def tile_binarylinear_pa_t_kernel(tc, x, W1, g1, b1, W2, g2, b2, out):
         load_w2(1)
 
         LANES = (
-            "matmul1", "x_transpose", "w_transpose",
+            "matmul1", "x_transpose", "w_transpose", "warm",
             "store", "relu2", "apply1", "x_copy", "sign", "norm2", "gain_shift", "regroup",
             "quantise", "stats1", "stats2", "matmul2", "transpose2",
         )
@@ -402,6 +412,10 @@ def tile_binarylinear_pa_t_kernel(tc, x, W1, g1, b1, W2, g2, b2, out):
             nc.vector.tensor_copy(out=vecs[:], in_=vec_bank[:, 0:n_vec_rows])
             nc.vector.tensor_scalar_mul(out=neg_vecs[:], in0=vec_bank[:, 0:n_vec_rows], scalar1=-1.0)
 
+        at(-2, "warm", keep_warm, 6)
+        at(-1, "warm", keep_warm, 2)
+        for c in range(N_CHUNKS):
+            at(c, "warm", keep_warm, 2 if c < 2 else 1)
         for half, slot in enumerate((-1, AT_W1_SECOND)):
             at(slot, "w_transpose", w1_transpose, half)
             at(slot, "sign", w1_sign, half)

@@ -24,20 +24,24 @@ WORDS = D_IN // 2
 STATS = 6
 
 
+GROUPS = ((0,), (1,), (2,), (3,), (4,), (5,), (6,), (7,))
 PAIR = 2
-N_GROUPS = T2 // PAIR
 
 AT_STATS1 = 2
-AT_STATS1_LATE = AT_STATS1 + N_CHUNKS
+AT_AFTER_X = AT_STATS1 + N_CHUNKS
 AT_W1_SECOND = N_CHUNKS
-AT_W2_SIGN = N_CHUNKS
-AT_APPLY1 = AT_STATS1_LATE + 3
+AT_W2_FIRST = AT_AFTER_X - 1
+AT_STATS1_LATE = AT_AFTER_X + 2
+AT_APPLY1 = AT_AFTER_X + 1
 VECTOR_APPLIES = 4
 AT_APPLY1_LATE = AT_APPLY1 + 3 * N_CHUNKS - VECTOR_APPLIES
 AT_REGROUP = AT_APPLY1_LATE + 1
 AT_LAYER2 = AT_REGROUP + 2
-LAG_NORM = 3
-LAG_TR = 2
+VNORM = lambda g, i, j: False
+WARM = ()
+SHARE = lambda m, c: m > 5
+LAG_PAIR = 1
+LAG_NORM = 2
 SCALAR_REGROUP_COLS = 128
 
 FLOPS = 2 * BATCH * D_IN * H1 + 2 * BATCH * H1 * H2
@@ -246,12 +250,11 @@ def tile_binarylinear_pa_t_kernel(tc, x, W1, g1, b1, W2, g2, b2, out):
                 func=ACT.Sign,
             )
 
-        def w2_quantise(half):
-            first, last = half * T2 // 2, (half + 1) * T2 // 2
+        def w2_quantise(m):
             nc.vector.quantize_mx(
-                out=w2_codes[:, first * P : last * P].bitcast(FP8X4),
-                scales=w2_scales[:, first * P : last * P],
-                in_=w2_grouped[:, first * PACK * P : last * PACK * P],
+                out=w2_codes[:, tile_cols(m)].bitcast(FP8X4),
+                scales=w2_scales[:, tile_cols(m)],
+                in_=w2_grouped[:, m * PACK * P : (m + 1) * PACK * P],
             )
 
         def layer1_matmul(use, t, c):
@@ -299,74 +302,85 @@ def tile_binarylinear_pa_t_kernel(tc, x, W1, g1, b1, W2, g2, b2, out):
                 in_=h_grouped[c][:],
             )
 
-        def group_tiles(g):
-            return range(g * PAIR, (g + 1) * PAIR)
+        def pieces(group):
+            n = N_CHUNKS * len(group) // PAIR
+            width = N_CHUNKS // n
+            return [range(i * width, (i + 1) * width) for i in range(n)]
 
-        def layer2_matmul(g, c):
-            for m in group_tiles(g):
-                bank = new_bank(F32)
-                nc.tensor.matmul_mx(
-                    out=bank[:],
-                    lhsT=w2_codes[:, tile_cols(m)].bitcast(FP8X4),
-                    lhsT_scale=w2_scales[:, tile_cols(m)],
-                    rhs=h_codes[:, chunk_cols(c)].bitcast(FP8X4),
-                    rhs_scale=h_scales[:, chunk_cols(c)],
-                    start=True,
-                    stop=True,
-                )
-                banks[("y2", m, c)] = bank
+        def layer2_matmul(group, chunks):
+            for m in group:
+                for c in chunks:
+                    bank = new_bank(F32)
+                    nc.tensor.matmul_mx(
+                        out=bank[:],
+                        lhsT=w2_codes[:, tile_cols(m)].bitcast(FP8X4),
+                        lhsT_scale=w2_scales[:, tile_cols(m)],
+                        rhs=h_codes[:, chunk_cols(c)].bitcast(FP8X4),
+                        rhs_scale=h_scales[:, chunk_cols(c)],
+                        start=True,
+                        stop=True,
+                    )
+                    banks[("y2", m, c)] = bank
 
-        def layer2_relu(g, c):
-            for m in group_tiles(g):
-                if c == 0:
-                    relu_tile = big.tile([P, BATCH], F32, name="relu_tile", tag="big")
-                    relu_y2[m] = relu_tile
-                nc.scalar.activation(
-                    out=relu_y2[m][:, chunk_cols(c)], in_=banks[("y2", m, c)][:], func=ACT.Relu
-                )
+        def layer2_relu(group, chunks):
+            for m in group:
+                for c in chunks:
+                    if c == 0:
+                        relu_tile = big.tile([P, BATCH], F32, name="relu_tile", tag="big")
+                        relu_y2[m] = relu_tile
+                    nc.scalar.activation(
+                        out=relu_y2[m][:, chunk_cols(c)], in_=banks[("y2", m, c)][:], func=ACT.Relu
+                    )
 
-        def layer2_stats(g, c):
-            for m in group_tiles(g):
-                nc.vector.bn_stats(out=stats2[:, m, c, :], in_=relu_y2[m][:, chunk_cols(c)])
-            if c == N_CHUNKS - 1:
-                norm_moments(2, stats2, g * PAIR, PAIR)
+        def layer2_stats(group, chunks):
+            for m in group:
+                for c in chunks:
+                    nc.vector.bn_stats(out=stats2[:, m, c, :], in_=relu_y2[m][:, chunk_cols(c)])
+            if chunks[-1] == N_CHUNKS - 1:
+                norm_moments(2, stats2, group[0], len(group))
 
-        def layer2_norm(g, c):
-            gain, shift = norms[(2, g * PAIR)]
-            for i, m in enumerate(group_tiles(g)):
-                piece = relu_y2[m][:, c * CHUNK : (c + 2) * CHUNK]
-                engine = nc.vector if g == N_GROUPS - 1 else nc.gpsimd
-                engine.tensor_scalar(
-                    out=piece,
-                    in0=piece,
-                    scalar1=gain[:, i : i + 1],
-                    scalar2=shift[:, i : i + 1],
-                    op0=ALU.mult,
-                    op1=ALU.add,
-                )
+        def layer2_norm(engine, group, chunks, i=0):
+            gain, shift = norms[(2, group[0])]
+            piece = relu_y2[group[i]][:, chunks[0] * CHUNK : (chunks[-1] + 1) * CHUNK]
+            engine.tensor_scalar(
+                out=piece,
+                in0=piece,
+                scalar1=gain[:, i : i + 1],
+                scalar2=shift[:, i : i + 1],
+                op0=ALU.mult,
+                op1=ALU.add,
+            )
 
-        def layer2_transpose(g, c):
+        def layer2_transpose(group, chunks):
+            squares = [
+                relu_y2[m][:, c * CHUNK + j * P : c * CHUNK + (j + 1) * P]
+                for c in chunks
+                for j in range(SUB)
+                for m in group
+            ]
             for half in range(2):
                 bank = new_bank(F32)
-                for jj in range(2):
-                    col = c * CHUNK + (2 * half + jj) * P
-                    for i, m in enumerate(group_tiles(g)):
-                        nc.tensor.transpose(
-                            out=bank[:, tile_cols(jj * PAIR + i)],
-                            in_=relu_y2[m][:, col : col + P],
-                            identity=ident_f[:],
-                        )
-                banks[("out", g, c, half)] = bank
+                for i in range(SUB):
+                    nc.tensor.transpose(
+                        out=bank[:, tile_cols(i)], in_=squares[half * SUB + i], identity=ident_f[:]
+                    )
+                banks[("out", group[0], chunks[0], half)] = bank
 
-        def layer2_store(g, c):
-            staged = staged_pool.tile([P, SUB * PAIR * P], F32, name="staged", tag="staged")
-            nc.scalar.copy(out=staged[:, 0:CHUNK], in_=banks[("out", g, c, 0)][:])
-            nc.vector.tensor_copy(out=staged[:, CHUNK : 2 * CHUNK], in_=banks[("out", g, c, 1)][:])
-            f0 = g * PAIR * P
-            nc.sync.dma_start(
-                out=out[chunk_cols(c), f0 : f0 + PAIR * P].rearrange("(p j) f -> p j f", j=SUB),
-                in_=staged[:].rearrange("p (j f) -> p j f", j=SUB),
-            )
+        def layer2_store(group, chunks):
+            staged = staged_pool.tile([P, 2 * CHUNK], F32, name="staged", tag="staged")
+            first, second = [banks[("out", group[0], chunks[0], half)] for half in range(2)]
+            nc.scalar.copy(out=staged[:, 0:CHUNK], in_=first[:])
+            if SHARE(group[0], chunks[0]):
+                nc.scalar.copy(out=staged[:, CHUNK : 2 * CHUNK], in_=second[:])
+            else:
+                nc.vector.tensor_copy(out=staged[:, CHUNK : 2 * CHUNK], in_=second[:])
+            width = SUB * len(group) * P
+            f0 = group[0] * P
+            for i, c in enumerate(chunks):
+                nc.sync.dma_start(
+                    out=out[chunk_cols(c), f0 : f0 + len(group) * P].rearrange("(p j) f -> p j f", j=SUB),
+                    in_=staged[:, i * width : (i + 1) * width].rearrange("p (j f) -> p j f", j=SUB),
+                )
 
         def load_w1(half):
             rows = slice(half * H1 // 2, (half + 1) * H1 // 2)
@@ -397,7 +411,7 @@ def tile_binarylinear_pa_t_kernel(tc, x, W1, g1, b1, W2, g2, b2, out):
         load_w2(1)
 
         LANES = (
-            "matmul1", "x_transpose", "w_transpose", "warm",
+            "x_transpose", "matmul1", "w_transpose", "warm",
             "store", "relu2", "apply1", "x_copy", "sign", "norm2", "gain_shift", "regroup",
             "quantise", "stats1", "stats2", "matmul2", "transpose2",
         )
@@ -406,9 +420,13 @@ def tile_binarylinear_pa_t_kernel(tc, x, W1, g1, b1, W2, g2, b2, out):
         def at(slot, lane, call, *args):
             agenda.setdefault(slot, []).append((LANES.index(lane), call, args))
 
-        def vectors():
+        def vectors_transpose():
             vec_bank = new_bank(BF16)
+            banks["vec"] = vec_bank
             nc.tensor.transpose(out=vec_bank[:, 0:P], in_=vec_rows[:], identity=ident_b[:])
+
+        def vectors_copy():
+            vec_bank = banks["vec"]
             nc.vector.tensor_copy(out=vecs[:], in_=vec_bank[:, 0:n_vec_rows])
             nc.vector.tensor_scalar_mul(out=neg_vecs[:], in0=vec_bank[:, 0:n_vec_rows], scalar1=-1.0)
 
@@ -416,52 +434,74 @@ def tile_binarylinear_pa_t_kernel(tc, x, W1, g1, b1, W2, g2, b2, out):
         at(-1, "warm", keep_warm, 2)
         for c in range(N_CHUNKS):
             at(c, "warm", keep_warm, 2 if c < 2 else 1)
+        for slot in WARM:
+            at(slot, "warm", keep_warm, 1)
         for half, slot in enumerate((-1, AT_W1_SECOND)):
             at(slot, "w_transpose", w1_transpose, half)
             at(slot, "sign", w1_sign, half)
             at(slot + half, "quantise", w1_quantise, half)
-        at(5, "w_transpose", vectors)
+        at(6, "w_transpose", vectors_transpose)
+        at(7, "quantise", vectors_copy)
         for c in range(N_CHUNKS):
             at(c, "x_transpose", x_transpose, c)
             at(c, "x_copy", x_copy, c)
             at(c + 1, "quantise", x_quantise, c)
-        for m in range(T2):
-            at(AT_W2_SIGN + m // 2, "w_transpose", w2_transpose, m)
-            at(AT_W2_SIGN + m // 2, "sign", w2_sign, m)
-            if m % (T2 // 2) == T2 // 2 - 1:
-                at(AT_W2_SIGN + m // 2 + 2, "quantise", w2_quantise, m // (T2 // 2))
         for t in range(T1):
             for c in range(N_CHUNKS):
-                slot = AT_STATS1 + c if t < 2 else AT_STATS1_LATE + (t - 2) * N_CHUNKS + c
+                if t == 0:
+                    slot = AT_STATS1 + c
+                elif t == 1:
+                    slot = AT_STATS1 + 2 + 2 * c if c < 4 else AT_AFTER_X + (c - 4) // 2
+                else:
+                    slot = AT_STATS1_LATE + (t - 2) * N_CHUNKS + c
                 at(slot, "matmul1", layer1_matmul, "stats1", t, c)
                 at(slot, "stats1", layer1_stats, t, c)
                 if c == N_CHUNKS - 1:
                     at(slot + 1, "gain_shift", norm_gain_shift, 1, t, 1)
                 on_vector = t == 2 and c < VECTOR_APPLIES
-                if t < 3:
+                if on_vector:
+                    slot = AT_STATS1_LATE + 2 * N_CHUNKS + c // 2
+                elif t < 3:
                     slot = AT_APPLY1 + t * N_CHUNKS + c - (VECTOR_APPLIES if t == 2 else 0)
                 else:
                     slot = AT_APPLY1_LATE + c
-                if on_vector:
-                    slot = AT_STATS1_LATE + 2 * N_CHUNKS + c // 2
                 at(slot, "matmul1", layer1_matmul, "apply1", t, c)
                 at(slot, "apply1", layer1_apply, t, c, on_vector)
         for c in range(N_CHUNKS):
             at(AT_REGROUP + c, "regroup", h_regroup, c)
             at(AT_REGROUP + c + 1, "quantise", h_quantise, c)
-        for g in range(N_GROUPS):
-            for c in range(N_CHUNKS):
-                slot = AT_LAYER2 + g * N_CHUNKS + c
-                at(slot - 1, "matmul2", layer2_matmul, g, c)
-                at(slot, "relu2", layer2_relu, g, c)
-                at(slot + 1, "stats2", layer2_stats, g, c)
-                if c == N_CHUNKS - 1:
-                    at(slot + 2, "gain_shift", norm_gain_shift, 2, g * PAIR, PAIR)
-                slot += N_CHUNKS + LAG_NORM
-                if c % 2 == 0:
-                    at(slot, "norm2", layer2_norm, g, c)
-                at(slot + LAG_TR, "transpose2", layer2_transpose, g, c)
-                at(slot + LAG_TR + 1, "store", layer2_store, g, c)
+        slot = AT_LAYER2
+        free = 0
+        for g, group in enumerate(GROUPS):
+            for i, m in enumerate(group):
+                w2_at = AT_W2_FIRST + i if g == 0 else slot - 4 + i
+                at(w2_at, "w_transpose", w2_transpose, m)
+                at(w2_at, "sign", w2_sign, m)
+                at(w2_at + 1, "quantise", w2_quantise, m)
+            for chunks in pieces(group):
+                if g == 0:
+                    slot = AT_LAYER2 + chunks[-1]
+                at(slot - 1, "matmul2", layer2_matmul, group, chunks)
+                at(slot, "relu2", layer2_relu, group, chunks)
+                at(slot + 1, "stats2", layer2_stats, group, chunks)
+                slot += 1
+            at(slot + 1, "gain_shift", norm_gain_shift, 2, group[0], len(group))
+            free = max(free, slot + LAG_NORM)
+            last = g == len(GROUPS) - 1
+            rate = len(group) if not last and len(GROUPS[g + 1]) == 1 else 1
+            for i, chunks in enumerate(pieces(group)):
+                norm_at, width = free + i // rate, len(chunks)
+                if len(group) == 2 and not last:
+                    norm_at, width = free + i // 2 * 2 // rate, 2 - i % 2 * 2
+                wide = range(chunks[0], chunks[0] + width)
+                for j in range(len(group)):
+                    if width:
+                        engine = nc.vector if last or VNORM(g, i, j) else nc.gpsimd
+                        at(norm_at, "norm2", layer2_norm, engine, group, wide, j)
+                lag = 1 if last else LAG_PAIR
+                at(free + i // rate + lag, "transpose2", layer2_transpose, group, chunks)
+                at(free + i // rate + lag + 1, "store", layer2_store, group, chunks)
+            free += len(pieces(group)) // rate
 
         for slot in sorted(agenda):
             for lane, call, args in sorted(agenda[slot], key=lambda entry: entry[0]):

from contextlib import ExitStack

import concourse.mybir as mybir
from concourse.masks import make_identity

F32 = mybir.dt.float32
BF16 = mybir.dt.bfloat16
U32 = mybir.dt.uint32
U8 = mybir.dt.uint8
FP8X4 = mybir.dt.float8_e4m3fn_x4
ACT = mybir.ActivationFunctionType
ALU = mybir.AluOpType

P = 128
PACK = 4
BATCH, D_IN, H1, H2 = 4096, 512, 512, 1024
EPS = 1e-5
CHUNK = 512
N_CHUNKS = BATCH // CHUNK
SUB = CHUNK // P
T1 = H1 // P
T2 = H2 // P
WORDS = D_IN // 2
STATS = 6


GROUPS = ((0,), (1,), (2,), (3,), (4,), (5,), (6,), (7,))
PAIR = 2

AT_STATS1 = 2
AT_AFTER_X = AT_STATS1 + N_CHUNKS
AT_W1_SECOND = N_CHUNKS
AT_W2_FIRST = AT_AFTER_X - 1
AT_STATS1_LATE = AT_AFTER_X + 2
AT_APPLY1 = AT_AFTER_X + 1
VECTOR_APPLIES = 4
AT_APPLY1_LATE = AT_APPLY1 + 3 * N_CHUNKS - VECTOR_APPLIES
AT_REGROUP = AT_APPLY1_LATE + 1
AT_LAYER2 = AT_REGROUP + 2
VNORM = lambda g, i, j: False
WARM = ()
SHARE = lambda m, c: m > 5
LAG_PAIR = 1
LAG_NORM = 2
SCALAR_REGROUP_COLS = 128

FLOPS = 2 * BATCH * D_IN * H1 + 2 * BATCH * H1 * H2


def tile_binarylinear_pa_t_kernel(tc, x, W1, g1, b1, W2, g2, b2, out):
    nc = tc.nc
    with ExitStack() as ctx:
        ctx.enter_context(tc.manual_schedule())
        keep = ctx.enter_context(tc.tile_pool(name="keep", bufs=1))
        psum = ctx.enter_context(tc.psum_pool(name="psum", bufs=8))

        def new_bank(dtype):
            return psum.tile([P, CHUNK], dtype, name="bank", tag="bank")

        def chunk_cols(c):
            return slice(c * CHUNK, (c + 1) * CHUNK)

        def tile_cols(t):
            return slice(t * P, (t + 1) * P)

        vec_rows = keep.tile([P, P], BF16, name="vec_rows")
        nc.vector.memset(vec_rows[:], 0.0)
        first_row = {}
        row = 0
        for key, vec in (("g1", g1), ("b1", b1), ("g2", g2), ("b2", b2)):
            n_rows = vec.shape[0] // P
            nc.scalar.dma_start(
                out=vec_rows[row : row + n_rows, :], in_=vec.rearrange("(r c) -> r c", c=P)
            )
            first_row[key] = row
            row += n_rows
        n_vec_rows = row
        vecs = keep.tile([P, n_vec_rows], F32, name="vecs")
        neg_vecs = keep.tile([P, n_vec_rows], F32, name="neg_vecs")
        minus_half = keep.tile([P, PAIR], F32, name="minus_half")
        nc.vector.memset(minus_half[:], -0.5)
        warm = keep.tile([P, 1], F32, name="warm")
        nc.scalar.activation(out=warm[:], in_=minus_half[:, 0:1], func=ACT.Sign)

        ident_f = keep.tile([P, P], F32, name="ident_f")
        make_identity(nc, ident_f[:])
        ident_b = keep.tile([P, P], BF16, name="ident_b")
        make_identity(nc, ident_b[:])

        big = ctx.enter_context(tc.tile_pool(name="big", bufs=6))
        grouped_pool = ctx.enter_context(tc.tile_pool(name="grouped", bufs=4))
        staged_pool = ctx.enter_context(tc.tile_pool(name="staged", bufs=4))

        def new_grouped():
            return grouped_pool.tile(
                [P, PACK * CHUNK], BF16, name="grouped", tag="grouped", align_bytes=64
            )

        weights = big.tile([P, (T1 + T2) * D_IN], BF16, name="weights", tag="big")
        w1_sb = weights[:, 0 : T1 * D_IN]
        w2_sb = weights[:, T1 * D_IN : (T1 + T2) * D_IN]
        x_tiles = []
        for half in range(2):
            x_half = big.tile([P, N_CHUNKS // 2 * SUB * D_IN], BF16, name="x_half", tag="big")
            x_tiles.append(x_half)

        def x_rows(c):
            i = c % (N_CHUNKS // 2)
            return x_tiles[c // (N_CHUNKS // 2)][:, i * SUB * D_IN : (i + 1) * SUB * D_IN]

        w1_grouped = keep.tile([P, PACK * H1], BF16, name="w1_grouped", align_bytes=64)
        w2_grouped = keep.tile([P, PACK * H2], BF16, name="w2_grouped", align_bytes=64)
        w1_codes = keep.tile([P, H1], U32, name="w1_codes", align_bytes=64)
        w1_scales = keep.tile([P, H1], U8, name="w1_scales", align_bytes=64)
        w2_codes = keep.tile([P, H2], U32, name="w2_codes", align_bytes=64)
        w2_scales = keep.tile([P, H2], U8, name="w2_scales", align_bytes=64)
        x_codes = keep.tile([P, BATCH], U32, name="x_codes", align_bytes=64)
        x_scales = keep.tile([P, BATCH], U8, name="x_scales", align_bytes=64)
        h_codes = keep.tile([P, BATCH], U32, name="h_codes", align_bytes=64)
        h_scales = keep.tile([P, BATCH], U8, name="h_scales", align_bytes=64)
        stats1 = keep.tile([P, T1, N_CHUNKS, STATS], F32, name="stats1")
        stats2 = keep.tile([P, T2, N_CHUNKS, STATS], F32, name="stats2")
        h_planes = keep.tile([P, T1, BATCH], BF16, name="h_planes")

        banks = {}
        norms = {}
        x_grouped = {}
        h_grouped = {}
        relu_y2 = {}

        zeros = keep.tile([P, CHUNK], BF16, name="zeros")
        nc.vector.memset(zeros[:], 0.0)

        def keep_warm(n):
            bank = new_bank(F32)
            for i in range(n):
                nc.tensor.matmul(
                    out=bank[:], lhsT=zeros[:, 0:P], rhs=zeros[:], start=True, stop=True
                )

        def transpose_words(words, half):
            bank = new_bank(F32)
            for tt in range(2):
                for u in range(2):
                    src = (2 * half + tt) * WORDS + u * P
                    dst = u * 2 * P + tt * P
                    nc.tensor.transpose(
                        out=bank[:, dst : dst + P],
                        in_=words[:, src : src + P],
                        identity=ident_f[:],
                    )
            return bank

        def norm_moments(layer, stats, first, n):
            mean_var = keep.tile([P, n, 2], F32, name="mean_var_%d_%d" % (layer, first))
            for i in range(n):
                nc.vector.bn_aggr(
                    out=mean_var[:, i, :],
                    in_=stats[:, first + i, :, :].rearrange("p c s -> p (c s)"),
                )
            norms[(layer, first)] = mean_var

        def norm_gain_shift(layer, first, n):
            label = "%d_%d" % (layer, first)
            g_col = first_row["g%d" % layer] + first
            b_col = first_row["b%d" % layer] + first
            gamma, neg_gamma = vecs[:, g_col : g_col + n], neg_vecs[:, g_col : g_col + n]
            mean_var = norms[(layer, first)]
            var_eps = keep.tile([P, n], F32, name="var_eps_" + label)
            nc.gpsimd.tensor_scalar(
                out=var_eps[:], in0=mean_var[:, :, 1], scalar1=EPS, scalar2=0.0, op0=ALU.add, op1=ALU.add
            )
            gamma_mean = keep.tile([P, n], F32, name="gamma_mean_" + label)
            nc.gpsimd.tensor_tensor(out=gamma_mean[:], in0=mean_var[:, :, 0], in1=neg_gamma, op=ALU.mult)
            rstd = keep.tile([P, n], F32, name="rstd_" + label)
            nc.gpsimd.tensor_tensor(out=rstd[:], in0=var_eps[:], in1=minus_half[:, 0:n], op=ALU.pow)
            gain = keep.tile([P, n], F32, name="gain_" + label)
            nc.gpsimd.tensor_tensor(out=gain[:], in0=rstd[:], in1=gamma, op=ALU.mult)
            shift = keep.tile([P, n], F32, name="shift_" + label)
            for i in range(n):
                nc.gpsimd.tensor_scalar(
                    out=shift[:, i : i + 1],
                    in0=rstd[:, i : i + 1],
                    scalar1=gamma_mean[:, i : i + 1],
                    scalar2=vecs[:, b_col + i : b_col + i + 1],
                    op0=ALU.mult,
                    op1=ALU.add,
                )
            norms[(layer, first)] = (gain, shift)

        def w1_transpose(half):
            banks[("w1", half)] = transpose_words(w1_sb.bitcast(F32), half)

        def w1_sign(half):
            width = 2 * P
            nc.scalar.activation(
                out=w1_grouped[:, half * PACK * width : (half + 1) * PACK * width].rearrange(
                    "p (w u e) -> p w u e", u=2, e=2
                ),
                in_=banks[("w1", half)][:].bitcast(BF16).rearrange("p (u w e) -> p w u e", u=2, e=2),
                func=ACT.Sign,
            )

        def w1_quantise(half):
            width = 2 * P
            cols = slice(half * width, (half + 1) * width)
            nc.vector.quantize_mx(
                out=w1_codes[:, cols].bitcast(FP8X4),
                scales=w1_scales[:, cols],
                in_=w1_grouped[:, half * PACK * width : (half + 1) * PACK * width],
            )

        def x_transpose(c):
            words = x_rows(c).bitcast(F32)
            banks[("x", c)] = [transpose_words(words, half) for half in range(2)]

        def x_copy(c):
            grouped = new_grouped()
            for half in range(2):
                dst = (
                    grouped[:]
                    .bitcast(F32)[:, half * CHUNK : (half + 1) * CHUNK]
                    .rearrange("p (w u) -> p w u", u=2)
                )
                src = banks[("x", c)][half][:].rearrange("p (u w) -> p w u", u=2)
                nc.scalar.copy(out=dst, in_=src)
            x_grouped[c] = grouped

        def x_quantise(c):
            nc.vector.quantize_mx(
                out=x_codes[:, chunk_cols(c)].bitcast(FP8X4),
                scales=x_scales[:, chunk_cols(c)],
                in_=x_grouped[c][:],
            )

        def w2_transpose(m):
            bank = new_bank(BF16)
            for t in range(PACK):
                nc.tensor.transpose(
                    out=bank[:, tile_cols(t)],
                    in_=w2_sb[:, m * H1 + t * P : m * H1 + (t + 1) * P],
                    identity=ident_b[:],
                )
            banks[("w2", m)] = bank

        def w2_sign(m):
            nc.scalar.activation(
                out=w2_grouped[:, m * PACK * P : (m + 1) * PACK * P],
                in_=banks[("w2", m)][:].rearrange("p (t f) -> p f t", t=PACK),
                func=ACT.Sign,
            )

        def w2_quantise(m):
            nc.vector.quantize_mx(
                out=w2_codes[:, tile_cols(m)].bitcast(FP8X4),
                scales=w2_scales[:, tile_cols(m)],
                in_=w2_grouped[:, m * PACK * P : (m + 1) * PACK * P],
            )

        def layer1_matmul(use, t, c):
            bank = new_bank(F32)
            nc.tensor.matmul_mx(
                out=bank[:],
                lhsT=w1_codes[:, tile_cols(t)].bitcast(FP8X4),
                lhsT_scale=w1_scales[:, tile_cols(t)],
                rhs=x_codes[:, chunk_cols(c)].bitcast(FP8X4),
                rhs_scale=x_scales[:, chunk_cols(c)],
                start=True,
                stop=True,
            )
            banks[(use, t, c)] = bank

        def layer1_stats(t, c):
            nc.vector.bn_stats(out=stats1[:, t, c, :], in_=banks[("stats1", t, c)][:])
            if c == N_CHUNKS - 1:
                norm_moments(1, stats1, t, 1)

        def layer1_apply(t, c, on_vector):
            gain, shift = norms[(1, t)]
            dst = h_planes[:, t, chunk_cols(c)]
            src = banks[("apply1", t, c)][:]
            if on_vector:
                nc.vector.tensor_scalar(
                    out=dst, in0=src, scalar1=gain[:], scalar2=shift[:], op0=ALU.mult, op1=ALU.add
                )
            else:
                nc.scalar.activation(out=dst, in_=src, func=ACT.Relu, scale=gain[:], bias=shift[:])

        def h_regroup(c):
            grouped = new_grouped()
            dst = grouped[:].rearrange("p (c i t) -> p c t i", i=4, t=PACK)
            src = h_planes[:, :, chunk_cols(c)].rearrange("p t (c i) -> p c t i", i=4)
            cut = (CHUNK - SCALAR_REGROUP_COLS) // 4
            nc.vector.tensor_scalar_max(out=dst[:, :cut], in0=src[:, :cut], scalar1=0.0)
            nc.scalar.activation(out=dst[:, cut:], in_=src[:, cut:], func=ACT.Relu)
            h_grouped[c] = grouped

        def h_quantise(c):
            nc.vector.quantize_mx(
                out=h_codes[:, chunk_cols(c)].bitcast(FP8X4),
                scales=h_scales[:, chunk_cols(c)],
                in_=h_grouped[c][:],
            )

        def pieces(group):
            n = N_CHUNKS * len(group) // PAIR
            width = N_CHUNKS // n
            return [range(i * width, (i + 1) * width) for i in range(n)]

        def layer2_matmul(group, chunks):
            for m in group:
                for c in chunks:
                    bank = new_bank(F32)
                    nc.tensor.matmul_mx(
                        out=bank[:],
                        lhsT=w2_codes[:, tile_cols(m)].bitcast(FP8X4),
                        lhsT_scale=w2_scales[:, tile_cols(m)],
                        rhs=h_codes[:, chunk_cols(c)].bitcast(FP8X4),
                        rhs_scale=h_scales[:, chunk_cols(c)],
                        start=True,
                        stop=True,
                    )
                    banks[("y2", m, c)] = bank

        def layer2_relu(group, chunks):
            for m in group:
                for c in chunks:
                    if c == 0:
                        relu_tile = big.tile([P, BATCH], F32, name="relu_tile", tag="big")
                        relu_y2[m] = relu_tile
                    nc.scalar.activation(
                        out=relu_y2[m][:, chunk_cols(c)], in_=banks[("y2", m, c)][:], func=ACT.Relu
                    )

        def layer2_stats(group, chunks):
            for m in group:
                for c in chunks:
                    nc.vector.bn_stats(out=stats2[:, m, c, :], in_=relu_y2[m][:, chunk_cols(c)])
            if chunks[-1] == N_CHUNKS - 1:
                norm_moments(2, stats2, group[0], len(group))

        def layer2_norm(engine, group, chunks, i=0):
            gain, shift = norms[(2, group[0])]
            piece = relu_y2[group[i]][:, chunks[0] * CHUNK : (chunks[-1] + 1) * CHUNK]
            engine.tensor_scalar(
                out=piece,
                in0=piece,
                scalar1=gain[:, i : i + 1],
                scalar2=shift[:, i : i + 1],
                op0=ALU.mult,
                op1=ALU.add,
            )

        def layer2_transpose(group, chunks):
            squares = [
                relu_y2[m][:, c * CHUNK + j * P : c * CHUNK + (j + 1) * P]
                for c in chunks
                for j in range(SUB)
                for m in group
            ]
            for half in range(2):
                bank = new_bank(F32)
                for i in range(SUB):
                    nc.tensor.transpose(
                        out=bank[:, tile_cols(i)], in_=squares[half * SUB + i], identity=ident_f[:]
                    )
                banks[("out", group[0], chunks[0], half)] = bank

        def layer2_store(group, chunks):
            staged = staged_pool.tile([P, 2 * CHUNK], F32, name="staged", tag="staged")
            first, second = [banks[("out", group[0], chunks[0], half)] for half in range(2)]
            nc.scalar.copy(out=staged[:, 0:CHUNK], in_=first[:])
            if SHARE(group[0], chunks[0]):
                nc.scalar.copy(out=staged[:, CHUNK : 2 * CHUNK], in_=second[:])
            else:
                nc.vector.tensor_copy(out=staged[:, CHUNK : 2 * CHUNK], in_=second[:])
            width = SUB * len(group) * P
            f0 = group[0] * P
            for i, c in enumerate(chunks):
                nc.sync.dma_start(
                    out=out[chunk_cols(c), f0 : f0 + len(group) * P].rearrange("(p j) f -> p j f", j=SUB),
                    in_=staged[:, i * width : (i + 1) * width].rearrange("p (j f) -> p j f", j=SUB),
                )

        def load_w1(half):
            rows = slice(half * H1 // 2, (half + 1) * H1 // 2)
            cols = slice(half * T1 // 2 * D_IN, (half + 1) * T1 // 2 * D_IN)
            nc.sync.dma_start(
                out=w1_sb[:, cols].rearrange("p (t k) -> p t k", k=D_IN),
                in_=W1[rows, :].rearrange("(t p) k -> p t k", p=P),
            )

        def load_x(c):
            nc.sync.dma_start(
                out=x_rows(c), in_=x[chunk_cols(c), :].rearrange("(p j) k -> p (j k)", j=SUB)
            )

        def load_w2(half):
            rows = slice(half * H2 // 2, (half + 1) * H2 // 2)
            cols = slice(half * T2 // 2 * H1, (half + 1) * T2 // 2 * H1)
            nc.sync.dma_start(
                out=w2_sb[:, cols].rearrange("p (m k) -> p m k", k=H1),
                in_=W2[rows, :].rearrange("(m p) k -> p m k", p=P),
            )

        load_w1(0)
        for c in range(N_CHUNKS):
            load_x(c)
        load_w1(1)
        load_w2(0)
        load_w2(1)

        LANES = (
            "x_transpose", "matmul1", "w_transpose", "warm",
            "store", "relu2", "apply1", "x_copy", "sign", "norm2", "gain_shift", "regroup",
            "quantise", "stats1", "stats2", "matmul2", "transpose2",
        )
        agenda = {}

        def at(slot, lane, call, *args):
            agenda.setdefault(slot, []).append((LANES.index(lane), call, args))

        def vectors_transpose():
            vec_bank = new_bank(BF16)
            banks["vec"] = vec_bank
            nc.tensor.transpose(out=vec_bank[:, 0:P], in_=vec_rows[:], identity=ident_b[:])

        def vectors_copy():
            vec_bank = banks["vec"]
            nc.vector.tensor_copy(out=vecs[:], in_=vec_bank[:, 0:n_vec_rows])
            nc.vector.tensor_scalar_mul(out=neg_vecs[:], in0=vec_bank[:, 0:n_vec_rows], scalar1=-1.0)

        at(-2, "warm", keep_warm, 6)
        at(-1, "warm", keep_warm, 2)
        for c in range(N_CHUNKS):
            at(c, "warm", keep_warm, 2 if c < 2 else 1)
        for slot in WARM:
            at(slot, "warm", keep_warm, 1)
        for half, slot in enumerate((-1, AT_W1_SECOND)):
            at(slot, "w_transpose", w1_transpose, half)
            at(slot, "sign", w1_sign, half)
            at(slot + half, "quantise", w1_quantise, half)
        at(6, "w_transpose", vectors_transpose)
        at(7, "quantise", vectors_copy)
        for c in range(N_CHUNKS):
            at(c, "x_transpose", x_transpose, c)
            at(c, "x_copy", x_copy, c)
            at(c + 1, "quantise", x_quantise, c)
        for t in range(T1):
            for c in range(N_CHUNKS):
                if t == 0:
                    slot = AT_STATS1 + c
                elif t == 1:
                    slot = AT_STATS1 + 2 + 2 * c if c < 4 else AT_AFTER_X + (c - 4) // 2
                else:
                    slot = AT_STATS1_LATE + (t - 2) * N_CHUNKS + c
                at(slot, "matmul1", layer1_matmul, "stats1", t, c)
                at(slot, "stats1", layer1_stats, t, c)
                if c == N_CHUNKS - 1:
                    at(slot + 1, "gain_shift", norm_gain_shift, 1, t, 1)
                on_vector = t == 2 and c < VECTOR_APPLIES
                if on_vector:
                    slot = AT_STATS1_LATE + 2 * N_CHUNKS + c // 2
                elif t < 3:
                    slot = AT_APPLY1 + t * N_CHUNKS + c - (VECTOR_APPLIES if t == 2 else 0)
                else:
                    slot = AT_APPLY1_LATE + c
                at(slot, "matmul1", layer1_matmul, "apply1", t, c)
                at(slot, "apply1", layer1_apply, t, c, on_vector)
        for c in range(N_CHUNKS):
            at(AT_REGROUP + c, "regroup", h_regroup, c)
            at(AT_REGROUP + c + 1, "quantise", h_quantise, c)
        slot = AT_LAYER2
        free = 0
        for g, group in enumerate(GROUPS):
            for i, m in enumerate(group):
                w2_at = AT_W2_FIRST + i if g == 0 else slot - 4 + i
                at(w2_at, "w_transpose", w2_transpose, m)
                at(w2_at, "sign", w2_sign, m)
                at(w2_at + 1, "quantise", w2_quantise, m)
            for chunks in pieces(group):
                if g == 0:
                    slot = AT_LAYER2 + chunks[-1]
                at(slot - 1, "matmul2", layer2_matmul, group, chunks)
                at(slot, "relu2", layer2_relu, group, chunks)
                at(slot + 1, "stats2", layer2_stats, group, chunks)
                slot += 1
            at(slot + 1, "gain_shift", norm_gain_shift, 2, group[0], len(group))
            free = max(free, slot + LAG_NORM)
            last = g == len(GROUPS) - 1
            rate = len(group) if not last and len(GROUPS[g + 1]) == 1 else 1
            for i, chunks in enumerate(pieces(group)):
                norm_at, width = free + i // rate, len(chunks)
                if len(group) == 2 and not last:
                    norm_at, width = free + i // 2 * 2 // rate, 2 - i % 2 * 2
                wide = range(chunks[0], chunks[0] + width)
                for j in range(len(group)):
                    if width:
                        engine = nc.vector if last or VNORM(g, i, j) else nc.gpsimd
                        at(norm_at, "norm2", layer2_norm, engine, group, wide, j)
                lag = 1 if last else LAG_PAIR
                at(free + i // rate + lag, "transpose2", layer2_transpose, group, chunks)
                at(free + i // rate + lag + 1, "store", layer2_store, group, chunks)
            free += len(pieces(group)) // rate

        for slot in sorted(agenda):
            for lane, call, args in sorted(agenda[slot], key=lambda entry: entry[0]):
                call(*args)
